import numpy as np
import ml_dtypes


def mxq(x, axis, fmt="e4m3"):
    dtype, down = {"e4m3": (ml_dtypes.float8_e4m3fn, 7), "e5m2": (ml_dtypes.float8_e5m2, 14)}[fmt]
    v = np.moveaxis(np.asarray(x, np.float32).astype(ml_dtypes.bfloat16).astype(np.float64), axis, -1)
    blocks = v.reshape(v.shape[:-1] + (-1, 32))
    amax = np.abs(blocks).max(-1, keepdims=True)
    byte = np.maximum(np.where(amax > 0, np.frexp(amax)[1] - 1 + 127, 0) - down, 1)
    scale = np.exp2(byte - 127.0)
    codes = (blocks / scale).astype(np.float32).astype(dtype).astype(np.float64)
    return np.moveaxis((codes * scale).reshape(v.shape), -1, axis)


WIDE = False


def mx_kscale(k):
    if not WIDE:
        return np.ones(k)
    levels = np.array([10, -10, 5, -5, 0])
    if k % 512:
        return np.exp2(np.random.permutation(np.resize(levels, k // 32))).repeat(32)
    a = np.empty((k // 512, 16))
    for p in range(k // 512):
        a[p, :8] = np.random.permutation(np.resize(levels, 8))
        for g in range(8):
            far = levels[np.abs(levels - a[p, g]) >= 10]
            a[p, g + 8] = far[np.random.randint(len(far))]
    return np.exp2(a.ravel()).repeat(32)


BF16 = ml_dtypes.bfloat16


def bf(x):
    return np.asarray(x, np.float32).astype(BF16)


def f64(x):
    return np.asarray(x).astype(np.float64)


M, N, H = 512, 1024, 2048
RMIN, RMAX = 0.4, 0.99


def half_glorot(rows, cols):
    limit = np.sqrt(1.5 / ((rows + cols) / 2.0))
    return np.random.uniform(-limit, limit, (rows, cols))


def draw0():
    s, t = mx_kscale(N), mx_kscale(H)
    inputs = np.random.standard_normal((M, N))
    state_re = np.random.standard_normal((M, H))
    state_im = np.random.standard_normal((M, H))
    C_re = half_glorot(H, N)
    C_im = half_glorot(H, N)
    B_re = half_glorot(N, H)
    B_im = half_glorot(N, H)
    D = np.random.standard_normal(N)
    nu = np.random.uniform(np.log(-np.log(RMAX)), np.log(-np.log(RMIN)), H)
    theta = np.random.uniform(0.0, 3.14 / 10, H)
    gamma = np.sqrt(1.0 - np.exp(-2.0 * np.exp(nu)))
    return {"inputs": bf(inputs * s), "state_re": bf(state_re * t), "state_im": bf(state_im * t),
            "B_re": bf(B_re / s[:, None]), "B_im": bf(B_im / s[:, None]),
            "C_re": bf(C_re / t[:, None]), "C_im": bf(C_im / t[:, None]),
            "D": bf(D / s), "nu": bf(nu), "theta": bf(theta), "gamma": bf(gamma * t)}


def core(inputs, state_re, state_im, B_re, B_im, C_re, C_im, D, nu, theta, gamma):
    u = f64(inputs)
    mag = np.exp(-np.exp(f64(nu)))
    lam_re = mag * np.cos(f64(theta))
    lam_im = mag * np.sin(f64(theta))
    uq = mxq(u, 1, "e4m3")
    new_u_re = f64(gamma) * (uq @ mxq(f64(B_re), 0, "e4m3"))
    new_u_im = f64(gamma) * (uq @ mxq(f64(B_im), 0, "e4m3"))
    x_re = f64(state_re) * lam_re - f64(state_im) * lam_im + new_u_re
    x_im = f64(state_re) * lam_im + f64(state_im) * lam_re + new_u_im
    y = (mxq(x_re, 1, "e4m3") @ mxq(f64(C_re), 0, "e4m3")) - (mxq(x_im, 1, "e4m3") @ mxq(f64(C_im), 0, "e4m3")) + f64(D) * u
    return y, x_re, x_im


def e4m3fn_bytes(y):
    return np.clip(np.asarray(y, np.float64), -448.0, 448.0).astype(np.float32).astype(ml_dtypes.float8_e4m3fn).view(np.uint8)


def e4m3fn_values(b):
    return np.asarray(b, np.uint8).view(ml_dtypes.float8_e4m3fn).astype(np.float64)


def setup_inputs():
    d = draw0()
    x0 = np.asarray(d['C_re']).astype(np.float64)
    s = (np.max(np.abs(x0), axis=(1,), keepdims=True) / 448.0).astype(np.float32)
    out = {}
    for k, v in d.items():
        if k == 'C_re':
            out['C_re_bytes'] = e4m3fn_bytes(x0 / s.astype(np.float64))
            out['C_re_scale'] = s
        else:
            out[k] = v
    return out


def reference(inputs, state_re, state_im, B_re, B_im, C_re_bytes, C_re_scale, C_im, D, nu, theta, gamma):
    return core(inputs, state_re, state_im, B_re, B_im, e4m3fn_values(C_re_bytes) * C_re_scale.astype(np.float64), C_im, D, nu, theta, gamma)

@@ -1,0 +1,437 @@
+import math
+from contextlib import ExitStack
+
+import concourse.mybir as mybir
+from concourse.masks import make_identity
+
+M, N, H = 512, 1024, 2048
+FLOPS = 8 * M * N * H
+
+F32 = mybir.dt.float32
+BF16 = mybir.dt.bfloat16
+U32 = mybir.dt.uint32
+I32 = mybir.dt.int32
+U8 = mybir.dt.uint8
+FP8 = mybir.dt.float8_e4m3fn
+FP8X4 = mybir.dt.float8_e4m3fn_x4
+Act = mybir.ActivationFunctionType
+Alu = mybir.AluOpType
+
+P = 128
+PACK = 4
+HB = 512
+BLOCKS = H // HB
+KP = N // 512
+MT = M // P
+RE, IM = 0, 1
+GRP = 6
+VBI = {(j, t, p) for j in (0, 1, 2) for t, p in ((3, 1),)} | {(1, 2, 1), (2, 2, 1)}
+LASTV = True
+
+
+def tile_linearrecurrentunitcell_kernel(tc, inputs, state_re, state_im, B_re, B_im, C_re_bytes, C_re_scale, C_im, D, nu, theta, gamma, out_0, out_1, out_2):
+    nc = tc.nc
+    states = (state_re, state_im)
+    Bs = (B_re, B_im)
+    outs = (out_1, out_2)
+
+    with ExitStack() as ctx:
+        keep = ctx.enter_context(tc.tile_pool(name="keep", bufs=1))
+        ring = ctx.enter_context(tc.tile_pool(name="ring", bufs=2))
+        psum = ctx.enter_context(tc.psum_pool(name="psum", bufs=1))
+
+        ident = keep.tile([P, P], F32, name="ident")
+        make_identity(nc, ident[:])
+
+        ctx.enter_context(tc.manual_schedule())
+
+        def small(vec, dtype, name):
+            t_ = keep.tile([P, BLOCKS, PACK], dtype, name=name)
+            nc.scalar.dma_start(out=t_[:], in_=vec.rearrange("(j p t) -> p j t", p=P, t=PACK))
+            return t_
+
+        nu_t = small(nu, BF16, "nu_t")
+        th_t = small(theta, BF16, "th_t")
+        ga_b = small(gamma, BF16, "ga_b")
+        cs_t = small(C_re_scale.rearrange("h o -> (h o)"), F32, "cs_t")
+
+        b_raw = {}
+
+        def load_b(j, r, g):
+            t_ = ring.tile([P, PACK, HB], BF16, tag="raw", bufs=9, name="b_raw", align_bytes=64)
+            nc.sync.dma_start(out=t_[:], in_=Bs[r].rearrange("(g p i) h -> g p i h", p=P, i=PACK)[g][:, :, j * HB:(j + 1) * HB])
+            b_raw[j, r, g] = t_
+
+        s_raw = {}
+
+        def load_s(j, r):
+            t_ = ring.tile([P, MT, HB], BF16, tag="s_raw", bufs=4, name="s_raw", align_bytes=64)
+            nc.sync.dma_start(out=t_[:], in_=states[r].rearrange("(a p) h -> p a h", p=P)[:, :, j * HB:(j + 1) * HB])
+            s_raw[j, r] = t_
+
+        u_sb = keep.tile([P, MT, N], BF16, name="u_sb", align_bytes=64)
+
+        def load_u(a):
+            nc.sync.dma_start(out=u_sb[:, a:a + 2, :], in_=inputs.rearrange("(a p) n -> p a n", p=P)[:, a:a + 2, :])
+
+        c_raw = {}
+
+        def load_c(j, r):
+            if r == IM:
+                t_ = ring.tile([P, PACK, N], BF16, tag="cim_raw", bufs=2, name="cim_raw", align_bytes=64)
+                nc.sync.dma_start(out=t_[:], in_=C_im.rearrange("(g p i) n -> g p i n", p=P, i=PACK)[j])
+            else:
+                t_ = ring.tile([P, PACK, N], U8, tag="cre_bytes", bufs=2, name="cre_bytes", align_bytes=64)
+                nc.sync.dma_start(out=t_[:], in_=C_re_bytes.rearrange("(g p i) n -> g p i n", p=P, i=PACK)[j])
+            c_raw[j, r] = t_
+
+        b_grp, b_codes = {}, {}
+
+        def bi(eng, j, r, g, part=None):
+            if part in (None, 0):
+                b_grp[j, r, g] = ring.tile([P, HB * PACK], BF16, tag="grp", bufs=GRP, name="b_grp", align_bytes=64)
+            sl = slice(0, PACK) if part is None else slice(2 * part, 2 * part + 2)
+            o = b_grp[j, r, g][:].rearrange("p (t m i) -> p t m i", t=PACK, i=PACK)[:, sl]
+            i = b_raw[j, r, g][:].rearrange("p i (m t) -> p t m i", t=PACK)[:, sl]
+            if eng == "v":
+                nc.vector.tensor_copy(out=o, in_=i)
+            else:
+                nc.scalar.copy(o, i)
+
+        def bq(j, r, g):
+            c = ring.tile([P, HB], U32, tag="b_codes", bufs=8, name="b_codes", align_bytes=64)
+            s = ring.tile([P, HB], U8, tag="b_scales", bufs=8, name="b_scales", align_bytes=64)
+            nc.vector.quantize_mx(out=c[:].bitcast(FP8X4), scales=s[:], in_=b_grp[j, r, g][:])
+            b_codes[j, r, g] = (c, s)
+
+        u_grp = [ring.tile([P, M, 2], F32, tag="grp", bufs=GRP, name=f"u_grp{g}", align_bytes=64) for g in range(KP)]
+        u_codes = []
+        for g in range(KP):
+            u_codes.append((keep.tile([P, M], U32, name=f"u_codes{g}", align_bytes=64), keep.tile([P, M], U8, name=f"u_scales{g}", align_bytes=64)))
+
+        u_ps = {}
+
+        def tu(g, a, bank):
+            b = psum.tile([P, 2, 256], F32, tag=bank, name="u_ps")
+            w = u_sb[:].bitcast(F32)
+            for i in range(2):
+                for q in range(2):
+                    nc.tensor.transpose(b[:, q, i * P:(i + 1) * P], w[:, a + i, 256 * g + q:256 * (g + 1):2], ident[:])
+            u_ps[g, a] = b
+
+        def eu(eng, g, a):
+            o = u_grp[g][:, a * P:(a + 2) * P, :]
+            i = u_ps[g, a][:].rearrange("p q r -> p r q")
+            if eng == "v":
+                nc.vector.tensor_copy(out=o, in_=i)
+            else:
+                nc.scalar.copy(o, i)
+
+        def uq(g):
+            nc.vector.quantize_mx(out=u_codes[g][0][:].bitcast(FP8X4), scales=u_codes[g][1][:], in_=u_grp[g][:].rearrange("p m q -> p (m q)").bitcast(BF16))
+
+        s_ps = {}
+
+        def ts(j, q):
+            for r in (RE, IM):
+                b = psum.tile([P, M], F32, tag=f"s{q}{r}", name="s_ps")
+                w = s_raw[j, r][:].bitcast(F32)
+                for a in range(MT):
+                    nc.tensor.transpose(b[:, a * P:(a + 1) * P], w[:, a, q::2], ident[:])
+                s_ps[j, q, r] = b
+
+        def sview(j, t, r):
+            return s_ps[j, t // 2, r][:].bitcast(BF16).rearrange("p (m e) -> p m e", e=2)[:, :, t % 2]
+
+        x = {}
+
+        def a1(j, t):
+            for r in (RE, IM):
+                if t == 0:
+                    x[j, r] = ring.tile([P, PACK, M], F32, tag=f"x{r}", bufs=2, name="x", align_bytes=64)
+                nc.scalar.activation(out=x[j, r][:, t, :], in_=sview(j, t, r), func=Act.Copy, scale=lr[:, j, t:t + 1])
+
+        def v2(j, t):
+            for r, coef in ((RE, nli), (IM, li)):
+                xt = x[j, r][:, t, :]
+                nc.vector.scalar_tensor_tensor(out=xt, in0=sview(j, t, 1 - r), scalar=coef[:, j, t:t + 1], in1=xt, op0=Alu.mult, op1=Alu.add)
+
+        p_ps = {}
+
+        def mm(j, t):
+            for r in (RE, IM):
+                b = psum.tile([P, M], F32, tag=f"p{r}", name="p_ps")
+                for g in range(KP):
+                    c, s = b_codes[j, r, g]
+                    nc.tensor.matmul_mx(out=b[:], lhsT=c[:, t * P:(t + 1) * P].bitcast(FP8X4), lhsT_scale=s[:, t * P:(t + 1) * P],
+                                        rhs=u_codes[g][0][:].bitcast(FP8X4), rhs_scale=u_codes[g][1][:], start=(g == 0), stop=(g == KP - 1))
+                p_ps[j, t, r] = b
+
+        def v3(j, t):
+            for r in (RE, IM):
+                xt = x[j, r][:, t, :]
+                nc.vector.scalar_tensor_tensor(out=xt, in0=p_ps[j, t, r][:], scalar=ga[:, j, t:t + 1], in1=xt, op0=Alu.mult, op1=Alu.add)
+
+        x_grp, x_codes = {}, {}
+        for j in range(BLOCKS):
+            for r in (RE, IM):
+                x_codes[j, r] = (keep.tile([P, M], U32, name=f"x_codes{j}{r}", align_bytes=64), keep.tile([P, M], U8, name=f"x_scales{j}{r}", align_bytes=64))
+
+        def cx(j, r):
+            t_ = ring.tile([P, HB * PACK], BF16, tag="grp", bufs=GRP, name="x_grp", align_bytes=64)
+            o = t_[:].rearrange("p (m t) -> p m t", t=PACK)
+            i = x[j, r][:].rearrange("p t m -> p m t")
+            if r == RE:
+                nc.vector.tensor_copy(out=o, in_=i)
+            else:
+                nc.vector.tensor_scalar(out=o, in0=i, scalar1=-1.0, scalar2=None, op0=Alu.mult)
+            x_grp[j, r] = t_
+
+        def qx(j, r):
+            c, s = x_codes[j, r]
+            nc.vector.quantize_mx(out=c[:].bitcast(FP8X4), scales=s[:], in_=x_grp[j, r][:])
+
+        o_n = [0]
+
+        def to(j, r, a):
+            b = psum.tile([P, PACK, P], F32, tag=f"o{o_n[0] % 2}", name="o_ps")
+            o_n[0] += 1
+            for t in range(PACK):
+                nc.tensor.transpose(b[:, t, :], x[j, r][:, t, a * P:(a + 1) * P], ident[:])
+            o = ring.tile([P, HB], F32, tag="o_sb", bufs=6, name="o_sb")
+            nc.scalar.copy(o[:].rearrange("p (c t) -> p c t", t=PACK), b[:].rearrange("p t c -> p c t"))
+            nc.sync.dma_start(out=outs[r][a * P:(a + 1) * P, j * HB:(j + 1) * HB], in_=o[:])
+
+        load_b(0, RE, 0)
+        load_u(0)
+        load_u(2)
+        load_b(0, RE, 1)
+        load_b(0, IM, 0)
+        load_b(0, IM, 1)
+        load_s(0, RE)
+        load_s(0, IM)
+        for r in (RE, IM):
+            for g in range(KP):
+                load_b(1, r, g)
+        load_s(1, RE)
+        load_s(1, IM)
+
+        def sm(name, dtype=F32):
+            return keep.tile([P, BLOCKS, PACK], dtype, name=name)
+
+        e1, mag, q, qi, qf, r1, r2, ab, carg, sh, ch, s2, sc, sc2, lr, li, nli, ga = [sm(n_, I32 if n_ == "qi" else F32) for n_ in
+            ("e1", "mag", "q", "qi", "qf", "r1", "r2", "ab", "carg", "sh", "ch", "s2", "sc", "sc2", "lr", "li", "nli", "ga")]
+        C1 = 6.28125
+        C2 = 2.0 * math.pi - C1
+        v = nc.vector
+        nc.scalar.activation(out=e1[:], in_=nu_t[:], func=Act.Exp)
+        nc.scalar.activation(out=mag[:], in_=e1[:], func=Act.Exp, scale=-1.0)
+        v.tensor_scalar(out=q[:], in0=th_t[:], scalar1=1.0 / (2.0 * math.pi), scalar2=None, op0=Alu.mult)
+        v.tensor_copy(out=qi[:], in_=q[:])
+        v.tensor_copy(out=qf[:], in_=qi[:])
+        v.scalar_tensor_tensor(out=r1[:], in0=qf[:], scalar=-C1, in1=th_t[:], op0=Alu.mult, op1=Alu.add)
+        v.scalar_tensor_tensor(out=r2[:], in0=qf[:], scalar=-C2, in1=r1[:], op0=Alu.mult, op1=Alu.add)
+        v.scalar_tensor_tensor(out=ab[:], in0=r2[:], scalar=-1.0, in1=r2[:], op0=Alu.mult, op1=Alu.max)
+        v.tensor_scalar(out=carg[:], in0=ab[:], scalar1=-0.5, scalar2=math.pi / 2.0, op0=Alu.mult, op1=Alu.add)
+        nc.scalar.activation(out=sh[:], in_=r2[:], func=Act.Sin, scale=0.5)
+        nc.scalar.activation(out=ch[:], in_=carg[:], func=Act.Sin)
+        v.tensor_copy(out=ga[:], in_=ga_b[:])
+
+        bi("v", 0, RE, 0)
+        tu(0, 0, "s00")
+        tu(1, 0, "s01")
+        tu(0, 2, "s10")
+        tu(1, 2, "s11")
+        eu("a", 0, 0)
+        eu("a", 1, 0)
+        eu("v", 0, 2)
+        eu("v", 1, 2)
+        bi("a", 0, RE, 1)
+        bq(0, RE, 0)
+        uq(0)
+        uq(1)
+        v.tensor_tensor(out=s2[:], in0=sh[:], in1=sh[:], op=Alu.mult)
+        v.scalar_tensor_tensor(out=sc[:], in0=sh[:], scalar=2.0, in1=ch[:], op0=Alu.mult, op1=Alu.mult)
+        v.tensor_scalar(out=sc2[:], in0=s2[:], scalar1=-2.0, scalar2=1.0, op0=Alu.mult, op1=Alu.add)
+        v.tensor_tensor(out=li[:], in0=sc[:], in1=mag[:], op=Alu.mult)
+        v.tensor_tensor(out=lr[:], in0=sc2[:], in1=mag[:], op=Alu.mult)
+        v.tensor_scalar(out=nli[:], in0=li[:], scalar1=-1.0, scalar2=None, op0=Alu.mult)
+        bi("v", 0, IM, 0)
+        bq(0, RE, 1)
+        bi("a", 0, IM, 1)
+        bq(0, IM, 0)
+        ts(0, 0)
+        ts(0, 1)
+        a1(0, 0)
+        bq(0, IM, 1)
+
+        def widen(j, h):
+            w = ring.tile([P, PACK, 512], BF16, tag="raw", bufs=9, name="c_w", align_bytes=64)
+            for t in range(PACK):
+                nc.scalar.activation(out=w[:, t, :], in_=c_raw[j, RE][:, t, h * 512:(h + 1) * 512].bitcast(FP8), func=Act.Copy, scale=cs_t[:, j, t:t + 1])
+            c_raw[j, "w", h] = w
+
+        c_grp, c_codes = {}, {}
+
+        def ci(eng, j, r, h):
+            t_ = ring.tile([P, HB * PACK], BF16, tag="grp", bufs=GRP, name="c_grp", align_bytes=64)
+            src = c_raw[j, "w", h][:] if r == RE else c_raw[j, IM][:, :, h * 512:(h + 1) * 512]
+            o = t_[:].rearrange("p (c n t) -> p c t n", n=4, t=PACK)
+            i = src.rearrange("p t (c n) -> p c t n", n=4)
+            if eng == "v":
+                nc.vector.tensor_copy(out=o, in_=i)
+            else:
+                nc.scalar.copy(o, i)
+            c_grp[j, r, h] = t_
+
+        def cq(j, r, h):
+            if h == 0:
+                c_codes[j, r] = (ring.tile([P, N], U32, tag="c_codes", bufs=4, name="c_codes", align_bytes=64), ring.tile([P, N], U8, tag="c_scales", bufs=4, name="c_scales", align_bytes=64))
+            c, s = c_codes[j, r]
+            nc.vector.quantize_mx(out=c[:, h * 512:(h + 1) * 512].bitcast(FP8X4), scales=s[:, h * 512:(h + 1) * 512], in_=c_grp[j, r, h][:])
+
+        d_b = keep.tile([P, N], BF16, name="d_b")
+        nc.sync.dma_start(out=d_b[:], in_=D.partition_broadcast(P))
+        du = keep.tile([P, MT, N], F32, name="du")
+
+        def dmul(k):
+            a, h = k // 2, k % 2
+            cols = slice(h * 512, (h + 1) * 512)
+            nc.vector.memset(du[:, a, h * 512:h * 512 + 1], 0.0)
+            return lambda: nc.gpsimd.tensor_tensor(out=du[:, a, cols], in0=u_sb[:, a, cols], in1=d_b[:, cols], op=Alu.mult)
+
+        y_tags = ["s00", "s01", "s10", "s11", "p0", "p1", "o0", "o1"]
+        banks = [(a, h) for h in range(2) for a in range(MT)]
+        y_ps = {}
+
+        def mm2(j, r, todo=None, first=False, last=False):
+            for b in (banks if todo is None else todo):
+                a, h = b
+                if first:
+                    y_ps[b] = psum.tile([P, 512], F32, tag=y_tags[banks.index(b)], name="y_ps")
+                xc, xs = x_codes[j, r]
+                c, s = c_codes[j, r]
+                nc.tensor.matmul_mx(out=y_ps[b][:], lhsT=xc[:, a * P:(a + 1) * P].bitcast(FP8X4), lhsT_scale=xs[:, a * P:(a + 1) * P],
+                                    rhs=c[:, h * 512:(h + 1) * 512].bitcast(FP8X4), rhs_scale=s[:, h * 512:(h + 1) * 512], start=first, stop=last)
+
+        PIECES = [(RE, 0), (RE, 1), (IM, 0), (IM, 1)]
+        L = BLOCKS - 1
+        for j in range(BLOCKS):
+            nxt = j + 1 < BLOCKS
+            prev = [(j - 1, r, a) for r in (RE, IM) for a in range(MT)] if j > 0 else []
+            for t in range(PACK):
+                if j + 2 < BLOCKS:
+                    if t in (1, 3):
+                        for g in range(KP):
+                            load_b(j + 2, RE if t == 1 else IM, g)
+                        load_s(j + 2, RE if t == 1 else IM)
+                if j == 2:
+                    if t < 2:
+                        load_c(t, IM)
+                        load_c(t, RE)
+                if t + 1 < PACK:
+                    a1(j, t + 1)
+                g_ = dmul((j - 1) * PACK + t) if j in (1, 2) else (lambda: None)
+                v2(j, t)
+                g_()
+                if t > 0:
+                    v3(j, t - 1)
+                elif j > 0:
+                    v3(j - 1, PACK - 1)
+                if t == 0:
+                    if j > 0:
+                        bq(j, *PIECES[3])
+                        cx(j - 1, RE)
+                elif nxt:
+                    bq(j + 1, *PIECES[t - 1])
+                if t == 2 and nxt:
+                    ts(j + 1, 0)
+                if t == 0 and j > 0:
+                    ts(j, 1)
+                for k in range(2):
+                    if prev:
+                        to(*prev.pop(0))
+                mm(j, t)
+                if t == 1 and j > 0:
+                    cx(j - 1, IM)
+                    qx(j - 1, RE)
+                if t == 2 and j > 0:
+                    qx(j - 1, IM)
+                if nxt:
+                    for part in range(2):
+                        bi("v" if (j, t, part) in VBI else "a", j + 1, *PIECES[t], part=part)
+                else:
+                    if t < 2:
+                        widen(0, t)
+                    if t == 2:
+                        ci("v", 0, IM, 0)
+                        ci("a", 1, IM, 0)
+                    if t == 3:
+                        ci("v", 0, IM, 1)
+                        cq(0, IM, 0)
+                        ci("a", 1, IM, 1)
+                if t == PACK - 1 and nxt:
+                    a1(j + 1, 0)
+
+        load_c(2, IM)
+        load_c(2, RE)
+        v3(L, PACK - 1)
+        cq(0, IM, 1)
+        ci("v", 0, RE, 0)
+        cq(1, IM, 0)
+        cx(L, RE)
+        cq(1, IM, 1)
+        to(L, RE, 0)
+        to(L, RE, 1)
+        widen(1, 0)
+        mm2(0, IM, banks[:6], True)
+        ci("v", 0, RE, 1)
+        cx(L, IM)
+        cq(0, RE, 0)
+        qx(L, RE)
+        to(L, RE, 2)
+        to(L, RE, 3)
+        widen(1, 1)
+        load_c(3, IM)
+        load_c(3, RE)
+        cq(0, RE, 1)
+        qx(L, IM)
+        for a in range(MT):
+            to(L, IM, a)
+        mm2(0, IM, banks[6:], True)
+        mm2(0, RE)
+        mm2(1, IM)
+        ci("v", 1, RE, 0)
+        ci("v", 1, RE, 1)
+        widen(2, 0)
+        widen(2, 1)
+        ci("v", 2, IM, 0)
+        cq(1, RE, 0)
+        ci("v", 2, IM, 1)
+        cq(1, RE, 1)
+        mm2(1, RE)
+        ci("a", 3, IM, 0)
+        widen(3, 0)
+        ci("v", 2, RE, 0)
+        cq(2, IM, 0)
+        ci("v", 2, RE, 1)
+        cq(2, IM, 1)
+        mm2(2, IM)
+        widen(3, 1)
+        ci("a", 3, IM, 1)
+        cq(2, RE, 0)
+        ci("v", 3, RE, 0)
+        cq(2, RE, 1)
+        mm2(2, RE)
+        ci("v" if LASTV else "a", 3, RE, 1)
+        cq(3, IM, 0)
+        cq(3, RE, 0)
+        cq(3, IM, 1)
+        mm2(3, IM)
+        cq(3, RE, 1)
+        for n_, b in enumerate(banks):
+            a, h = b
+            mm2(3, RE, [b], False, True)
+            y = ring.tile([P, 512], F32, tag="o_sb", bufs=6, name="y_sb")
+            nc.vector.tensor_tensor(out=y[:], in0=y_ps[b][:], in1=du[:, a, h * 512:(h + 1) * 512], op=Alu.add)
+            nc.sync.dma_start(out=out_0[a * P:(a + 1) * P, h * 512:(h + 1) * 512], in_=y[:])

@@ -45,15 +45,13 @@ def tile_linearrecurrentunitcell_kernel(tc, inputs, state_re, state_im, B_re, B_
 
         ctx.enter_context(tc.manual_schedule())
 
-        def small(vec, dtype, name):
-            t_ = keep.tile([P, BLOCKS, PACK], dtype, name=name)
-            nc.scalar.dma_start(out=t_[:], in_=vec.rearrange("(j p t) -> p j t", p=P, t=PACK))
-            return t_
-
-        nu_t = small(nu, BF16, "nu_t")
-        th_t = small(theta, BF16, "th_t")
-        ga_b = small(gamma, BF16, "ga_b")
-        cs_t = small(C_re_scale.rearrange("h o -> (h o)"), F32, "cs_t")
+        cs_t = keep.tile([P, BLOCKS, PACK], F32, name="cs_t")
+        ident_b = keep.tile([P, P], BF16, name="ident_b")
+        lv = keep.tile([P, HB], BF16, name="lv")
+        nc.vector.memset(lv[:], 0.0)
+        nc.vector.tensor_copy(out=ident_b[:], in_=ident[:])
+        for n_, vec in enumerate((nu, theta, gamma)):
+            nc.scalar.dma_start(out=lv[BLOCKS * n_:BLOCKS * (n_ + 1), :], in_=vec.rearrange("(j c) -> j c", j=BLOCKS))
 
         b_raw = {}
 
@@ -90,9 +88,9 @@ def tile_linearrecurrentunitcell_kernel(tc, inputs, state_re, state_im, B_re, B_
         def bi(eng, j, r, g, part=None):
             if part in (None, 0):
                 b_grp[j, r, g] = ring.tile([P, HB * PACK], BF16, tag="grp", bufs=GRP, name="b_grp", align_bytes=64)
-            sl = slice(0, PACK) if part is None else slice(2 * part, 2 * part + 2)
-            o = b_grp[j, r, g][:].rearrange("p (t m i) -> p t m i", t=PACK, i=PACK)[:, sl]
-            i = b_raw[j, r, g][:].rearrange("p i (m t) -> p t m i", t=PACK)[:, sl]
+            sl = slice(0, P) if part is None else slice(64 * part, 64 * part + 64)
+            o = b_grp[j, r, g][:].rearrange("p (t m i) -> p m i t", t=PACK, i=PACK)[:, sl]
+            i = b_raw[j, r, g][:].rearrange("p i (m t) -> p m i t", t=PACK)[:, sl]
             if eng == "v":
                 nc.vector.tensor_copy(out=o, in_=i)
             else:
@@ -149,17 +147,17 @@ def tile_linearrecurrentunitcell_kernel(tc, inputs, state_re, state_im, B_re, B_
             for r in (RE, IM):
                 if t == 0:
                     x[j, r] = ring.tile([P, PACK, M], F32, tag=f"x{r}", bufs=2, name="x", align_bytes=64)
-                nc.scalar.activation(out=x[j, r][:, t, :], in_=sview(j, t, r), func=Act.Copy, scale=lr[:, j, t:t + 1])
+                nc.scalar.activation(out=x[j, r][:, t, :], in_=sview(j, t, r), func=Act.Copy, scale=lr[:, t, j:j + 1])
 
         def v2(j, t):
             for r, coef in ((RE, nli), (IM, li)):
                 xt = x[j, r][:, t, :]
-                nc.vector.scalar_tensor_tensor(out=xt, in0=sview(j, t, 1 - r), scalar=coef[:, j, t:t + 1], in1=xt, op0=Alu.mult, op1=Alu.add)
+                nc.vector.scalar_tensor_tensor(out=xt, in0=sview(j, t, 1 - r), scalar=coef[:, t, j:j + 1], in1=xt, op0=Alu.mult, op1=Alu.add)
 
         p_ps = {}
 
-        def mm(j, t):
-            for r in (RE, IM):
+        def mm(j, t, rs=(RE, IM)):
+            for r in rs:
                 b = psum.tile([P, M], F32, tag=f"p{r}", name="p_ps")
                 for g in range(KP):
                     c, s = b_codes[j, r, g]
@@ -170,7 +168,7 @@ def tile_linearrecurrentunitcell_kernel(tc, inputs, state_re, state_im, B_re, B_
         def v3(j, t):
             for r in (RE, IM):
                 xt = x[j, r][:, t, :]
-                nc.vector.scalar_tensor_tensor(out=xt, in0=p_ps[j, t, r][:], scalar=ga[:, j, t:t + 1], in1=xt, op0=Alu.mult, op1=Alu.add)
+                nc.vector.scalar_tensor_tensor(out=xt, in0=p_ps[j, t, r][:], scalar=ga[:, t, j:j + 1], in1=xt, op0=Alu.mult, op1=Alu.add)
 
         x_grp, x_codes = {}, {}
         for j in range(BLOCKS):
@@ -179,8 +177,8 @@ def tile_linearrecurrentunitcell_kernel(tc, inputs, state_re, state_im, B_re, B_
 
         def cx(j, r):
             t_ = ring.tile([P, HB * PACK], BF16, tag="grp", bufs=GRP, name="x_grp", align_bytes=64)
-            o = t_[:].rearrange("p (m t) -> p m t", t=PACK)
-            i = x[j, r][:].rearrange("p t m -> p m t")
+            o = t_[:].rearrange("p (c n t) -> p c t n", n=4, t=PACK)
+            i = x[j, r][:].rearrange("p t (c n) -> p c t n", n=4)
             if r == RE:
                 nc.vector.tensor_copy(out=o, in_=i)
             else:
@@ -217,53 +215,56 @@ def tile_linearrecurrentunitcell_kernel(tc, inputs, state_re, state_im, B_re, B_
         load_s(1, IM)
 
         def sm(name, dtype=F32):
-            return keep.tile([P, BLOCKS, PACK], dtype, name=name)
+            return keep.tile([P, PACK, BLOCKS], dtype, name=name)
 
-        e1, mag, q, qi, qf, r1, r2, ab, carg, sh, ch, s2, sc, sc2, lr, li, nli, ga = [sm(n_, I32 if n_ == "qi" else F32) for n_ in
-            ("e1", "mag", "q", "qi", "qf", "r1", "r2", "ab", "carg", "sh", "ch", "s2", "sc", "sc2", "lr", "li", "nli", "ga")]
+        e1, mag, qi, r1, r2, ab, carg, sh, ch, s2, sc, sc2, lr, li, nli = [sm(n_, I32 if n_ == "qi" else F32) for n_ in
+            ("e1", "mag", "qi", "r1", "r2", "ab", "carg", "sh", "ch", "s2", "sc", "sc2", "lr", "li", "nli")]
         C1 = 6.28125
         C2 = 2.0 * math.pi - C1
         v = nc.vector
-        nc.scalar.activation(out=e1[:], in_=nu_t[:], func=Act.Exp)
+        v_ps = psum.tile([P, PACK, P], BF16, tag="p0", name="v_ps")
+        for t in range(PACK):
+            nc.tensor.transpose(v_ps[:, t, :], lv[:, t::PACK], ident_b[:])
+        sv = keep.tile([P, PACK, 3 * BLOCKS], F32, name="sv")
+        v.tensor_copy(out=sv[:], in_=v_ps[:, :, 0:3 * BLOCKS])
+        th = sv[:, :, BLOCKS:2 * BLOCKS]
+        ga = sv[:, :, 2 * BLOCKS:3 * BLOCKS]
+        nc.scalar.activation(out=e1[:], in_=sv[:, :, 0:BLOCKS], func=Act.Exp)
         nc.scalar.activation(out=mag[:], in_=e1[:], func=Act.Exp, scale=-1.0)
-        v.tensor_scalar(out=q[:], in0=th_t[:], scalar1=1.0 / (2.0 * math.pi), scalar2=None, op0=Alu.mult)
-        v.tensor_copy(out=qi[:], in_=q[:])
-        v.tensor_copy(out=qf[:], in_=qi[:])
-        v.scalar_tensor_tensor(out=r1[:], in0=qf[:], scalar=-C1, in1=th_t[:], op0=Alu.mult, op1=Alu.add)
-        v.scalar_tensor_tensor(out=r2[:], in0=qf[:], scalar=-C2, in1=r1[:], op0=Alu.mult, op1=Alu.add)
-        v.scalar_tensor_tensor(out=ab[:], in0=r2[:], scalar=-1.0, in1=r2[:], op0=Alu.mult, op1=Alu.max)
-        v.tensor_scalar(out=carg[:], in0=ab[:], scalar1=-0.5, scalar2=math.pi / 2.0, op0=Alu.mult, op1=Alu.add)
-        nc.scalar.activation(out=sh[:], in_=r2[:], func=Act.Sin, scale=0.5)
-        nc.scalar.activation(out=ch[:], in_=carg[:], func=Act.Sin)
-        v.tensor_copy(out=ga[:], in_=ga_b[:])
-
+        v.tensor_scalar(out=qi[:], in0=th, scalar1=1.0 / (2.0 * math.pi), scalar2=None, op0=Alu.mult)
+        v.scalar_tensor_tensor(out=r1[:], in0=qi[:], scalar=-C1, in1=th, op0=Alu.mult, op1=Alu.add)
         bi("v", 0, RE, 0)
+        v.scalar_tensor_tensor(out=r2[:], in0=qi[:], scalar=-C2, in1=r1[:], op0=Alu.mult, op1=Alu.add)
         tu(0, 0, "s00")
         tu(1, 0, "s01")
         tu(0, 2, "s10")
         tu(1, 2, "s11")
         eu("a", 0, 0)
         eu("a", 1, 0)
-        eu("v", 0, 2)
-        eu("v", 1, 2)
-        bi("a", 0, RE, 1)
+        eu("a", 0, 2)
+        eu("a", 1, 2)
         bq(0, RE, 0)
+        v.scalar_tensor_tensor(out=ab[:], in0=r2[:], scalar=-1.0, in1=r2[:], op0=Alu.mult, op1=Alu.max)
+        bi("v", 0, RE, 1)
+        v.tensor_scalar(out=carg[:], in0=ab[:], scalar1=-0.5, scalar2=math.pi / 2.0, op0=Alu.mult, op1=Alu.add)
+        nc.scalar.activation(out=sh[:], in_=r2[:], func=Act.Sin, scale=0.5)
+        nc.scalar.activation(out=ch[:], in_=carg[:], func=Act.Sin)
         uq(0)
+        bq(0, RE, 1)
         uq(1)
+        bi("a", 0, IM, 0)
+        ts(0, 0)
         v.tensor_tensor(out=s2[:], in0=sh[:], in1=sh[:], op=Alu.mult)
         v.scalar_tensor_tensor(out=sc[:], in0=sh[:], scalar=2.0, in1=ch[:], op0=Alu.mult, op1=Alu.mult)
         v.tensor_scalar(out=sc2[:], in0=s2[:], scalar1=-2.0, scalar2=1.0, op0=Alu.mult, op1=Alu.add)
         v.tensor_tensor(out=li[:], in0=sc[:], in1=mag[:], op=Alu.mult)
         v.tensor_tensor(out=lr[:], in0=sc2[:], in1=mag[:], op=Alu.mult)
+        bi("v", 0, IM, 1)
         v.tensor_scalar(out=nli[:], in0=li[:], scalar1=-1.0, scalar2=None, op0=Alu.mult)
-        bi("v", 0, IM, 0)
-        bq(0, RE, 1)
-        bi("a", 0, IM, 1)
-        bq(0, IM, 0)
-        ts(0, 0)
-        ts(0, 1)
         a1(0, 0)
+        bq(0, IM, 0)
         bq(0, IM, 1)
+        ts(0, 1)
 
         def widen(j, h):
             w = ring.tile([P, PACK, 512], BF16, tag="raw", bufs=9, name="c_w", align_bytes=64)
@@ -292,6 +293,7 @@ def tile_linearrecurrentunitcell_kernel(tc, inputs, state_re, state_im, B_re, B_
 
         d_b = keep.tile([P, N], BF16, name="d_b")
         nc.sync.dma_start(out=d_b[:], in_=D.partition_broadcast(P))
+        nc.sync.dma_start(out=cs_t[:], in_=C_re_scale.rearrange("(j p t) o -> p j (t o)", p=P, t=PACK))
         du = keep.tile([P, MT, N], F32, name="du")
 
         def dmul(k):

@@ -19,14 +19,16 @@ Alu = mybir.AluOpType
 
 P = 128
 PACK = 4
-HB = 512
-BLOCKS = H // HB
-KP = N // 512
+W = P * PACK
+BLOCKS = H // W
+KP = N // W
 MT = M // P
 RE, IM = 0, 1
-GRP = 6
-VBI = {(j, t, p) for j in (0, 1, 2) for t, p in ((3, 1),)} | {(1, 2, 1), (2, 2, 1)}
-LASTV = True
+RAW, GRP, BC, OB, CC = 8, 7, 7, 5, 5
+PIECES = [(RE, 0), (RE, 1), (IM, 0), (IM, 1)]
+VBI = {(0, 2), (1, 2), (2, 2)}
+GP = 5
+VCI = {(0, RE, 0), (0, RE, 1), (1, RE, 0), (1, RE, 1), (2, RE, 0), (2, RE, 1), (3, RE, 0), (3, RE, 1)}
 
 
 def tile_linearrecurrentunitcell_kernel(tc, inputs, state_re, state_im, B_re, B_im, C_re_bytes, C_re_scale, C_im, D, nu, theta, gamma, out_0, out_1, out_2):
@@ -39,74 +41,84 @@ def tile_linearrecurrentunitcell_kernel(tc, inputs, state_re, state_im, B_re, B_
         keep = ctx.enter_context(tc.tile_pool(name="keep", bufs=1))
         ring = ctx.enter_context(tc.tile_pool(name="ring", bufs=2))
         psum = ctx.enter_context(tc.psum_pool(name="psum", bufs=1))
-
-        ident = keep.tile([P, P], F32, name="ident")
-        make_identity(nc, ident[:])
-
         ctx.enter_context(tc.manual_schedule())
+        v = nc.vector
 
-        cs_t = keep.tile([P, BLOCKS, PACK], F32, name="cs_t")
-        ident_b = keep.tile([P, P], BF16, name="ident_b")
-        lv = keep.tile([P, HB], BF16, name="lv")
-        nc.vector.memset(lv[:], 0.0)
-        nc.vector.tensor_copy(out=ident_b[:], in_=ident[:])
+        lv = keep.tile([P, W], BF16, name="lv")
+        v.memset(lv[:], 0.0)
         for n_, vec in enumerate((nu, theta, gamma)):
-            nc.scalar.dma_start(out=lv[BLOCKS * n_:BLOCKS * (n_ + 1), :], in_=vec.rearrange("(j c) -> j c", j=BLOCKS))
+            nc.sync.dma_start(out=lv[BLOCKS * n_:BLOCKS * (n_ + 1), :], in_=vec.rearrange("(j c) -> j c", j=BLOCKS))
 
-        b_raw = {}
+        b_raw, s_raw, c_raw = {}, {}, {}
 
         def load_b(j, r, g):
-            t_ = ring.tile([P, PACK, HB], BF16, tag="raw", bufs=9, name="b_raw", align_bytes=64)
-            nc.sync.dma_start(out=t_[:], in_=Bs[r].rearrange("(g p i) h -> g p i h", p=P, i=PACK)[g][:, :, j * HB:(j + 1) * HB])
-            b_raw[j, r, g] = t_
-
-        s_raw = {}
+            b_raw[j, r, g] = ring.tile([P, PACK, W], BF16, tag="raw", bufs=RAW, name="b_raw", align_bytes=64)
+            nc.sync.dma_start(out=b_raw[j, r, g][:], in_=Bs[r].rearrange("(g p i) h -> g p i h", p=P, i=PACK)[g][:, :, j * W:(j + 1) * W])
 
         def load_s(j, r):
-            t_ = ring.tile([P, MT, HB], BF16, tag="s_raw", bufs=4, name="s_raw", align_bytes=64)
-            nc.sync.dma_start(out=t_[:], in_=states[r].rearrange("(a p) h -> p a h", p=P)[:, :, j * HB:(j + 1) * HB])
-            s_raw[j, r] = t_
+            s_raw[j, r] = ring.tile([P, MT, W], BF16, tag="s_raw", bufs=4, name="s_raw", align_bytes=64)
+            nc.sync.dma_start(out=s_raw[j, r][:], in_=states[r].rearrange("(a p) h -> p a h", p=P)[:, :, j * W:(j + 1) * W])
 
         u_sb = keep.tile([P, MT, N], BF16, name="u_sb", align_bytes=64)
 
         def load_u(a):
             nc.sync.dma_start(out=u_sb[:, a:a + 2, :], in_=inputs.rearrange("(a p) n -> p a n", p=P)[:, a:a + 2, :])
 
-        c_raw = {}
+        def load_cim(j):
+            c_raw[j, IM] = ring.tile([P, PACK, N], BF16, tag="cim_raw", bufs=2, name="cim_raw", align_bytes=64)
+            nc.sync.dma_start(out=c_raw[j, IM][:], in_=C_im.rearrange("(g p i) n -> g p i n", p=P, i=PACK)[j])
 
-        def load_c(j, r):
-            if r == IM:
-                t_ = ring.tile([P, PACK, N], BF16, tag="cim_raw", bufs=2, name="cim_raw", align_bytes=64)
-                nc.sync.dma_start(out=t_[:], in_=C_im.rearrange("(g p i) n -> g p i n", p=P, i=PACK)[j])
-            else:
-                t_ = ring.tile([P, PACK, N], U8, tag="cre_bytes", bufs=2, name="cre_bytes", align_bytes=64)
-                nc.sync.dma_start(out=t_[:], in_=C_re_bytes.rearrange("(g p i) n -> g p i n", p=P, i=PACK)[j])
-            c_raw[j, r] = t_
+        def load_cre(j):
+            c_raw[j, RE] = ring.tile([P, PACK, N], U8, tag="cre_bytes", bufs=2, name="cre_bytes", align_bytes=64)
+            nc.sync.dma_start(out=c_raw[j, RE][:], in_=C_re_bytes.rearrange("(g p i) n -> g p i n", p=P, i=PACK)[j])
 
-        b_grp, b_codes = {}, {}
+        d_b = keep.tile([P, N], BF16, name="d_b")
+        cs_t = keep.tile([P, BLOCKS, PACK], F32, name="cs_t")
 
-        def bi(eng, j, r, g, part=None):
-            if part in (None, 0):
-                b_grp[j, r, g] = ring.tile([P, HB * PACK], BF16, tag="grp", bufs=GRP, name="b_grp", align_bytes=64)
-            sl = slice(0, P) if part is None else slice(64 * part, 64 * part + 64)
-            o = b_grp[j, r, g][:].rearrange("p (t m i) -> p m i t", t=PACK, i=PACK)[:, sl]
-            i = b_raw[j, r, g][:].rearrange("p i (m t) -> p m i t", t=PACK)[:, sl]
+        load_b(0, RE, 0)
+        load_u(0)
+        load_u(2)
+        load_b(0, RE, 1)
+        load_b(0, IM, 0)
+        load_b(0, IM, 1)
+        load_s(0, RE)
+        load_s(0, IM)
+        nc.sync.dma_start(out=d_b[:], in_=D.partition_broadcast(P))
+        for r in (RE, IM):
+            for g in range(KP):
+                load_b(1, r, g)
+        load_s(1, RE)
+        load_s(1, IM)
+        load_cim(0)
+
+        ident = keep.tile([P, P], F32, name="ident")
+        make_identity(nc, ident[:])
+        ident_b = keep.tile([P, P], BF16, name="ident_b")
+        v.tensor_copy(out=ident_b[:], in_=ident[:])
+
+        def copy(eng, o, i):
             if eng == "v":
-                nc.vector.tensor_copy(out=o, in_=i)
+                v.tensor_copy(out=o, in_=i)
             else:
                 nc.scalar.copy(o, i)
 
+        def grp(name):
+            return ring.tile([P, W * PACK], BF16, tag="grp", bufs=GRP, name=name, align_bytes=64)
+
+        b_grp, b_codes = {}, {}
+
+        def bi(eng, j, r, g):
+            b_grp[j, r, g] = grp("b_grp")
+            copy(eng, b_grp[j, r, g][:].rearrange("p (t m i) -> p m i t", t=PACK, i=PACK), b_raw[j, r, g][:].rearrange("p i (m t) -> p m i t", t=PACK))
+
         def bq(j, r, g):
-            c = ring.tile([P, HB], U32, tag="b_codes", bufs=8, name="b_codes", align_bytes=64)
-            s = ring.tile([P, HB], U8, tag="b_scales", bufs=8, name="b_scales", align_bytes=64)
-            nc.vector.quantize_mx(out=c[:].bitcast(FP8X4), scales=s[:], in_=b_grp[j, r, g][:])
+            c = ring.tile([P, W], U32, tag="b_codes", bufs=BC, name="b_codes", align_bytes=64)
+            s = ring.tile([P, W], U8, tag="b_scales", bufs=BC, name="b_scales", align_bytes=64)
+            v.quantize_mx(out=c[:].bitcast(FP8X4), scales=s[:], in_=b_grp[j, r, g][:])
             b_codes[j, r, g] = (c, s)
 
-        u_grp = [ring.tile([P, M, 2], F32, tag="grp", bufs=GRP, name=f"u_grp{g}", align_bytes=64) for g in range(KP)]
-        u_codes = []
-        for g in range(KP):
-            u_codes.append((keep.tile([P, M], U32, name=f"u_codes{g}", align_bytes=64), keep.tile([P, M], U8, name=f"u_scales{g}", align_bytes=64)))
-
+        u_grp = [grp("u_grp") for _ in range(KP)]
+        u_codes = [(keep.tile([P, M], U32, name=f"u_codes{g}", align_bytes=64), keep.tile([P, M], U8, name=f"u_scales{g}", align_bytes=64)) for g in range(KP)]
         u_ps = {}
 
         def tu(g, a, bank):
@@ -118,17 +130,12 @@ def tile_linearrecurrentunitcell_kernel(tc, inputs, state_re, state_im, B_re, B_
             u_ps[g, a] = b
 
         def eu(eng, g, a):
-            o = u_grp[g][:, a * P:(a + 2) * P, :]
-            i = u_ps[g, a][:].rearrange("p q r -> p r q")
-            if eng == "v":
-                nc.vector.tensor_copy(out=o, in_=i)
-            else:
-                nc.scalar.copy(o, i)
+            copy(eng, u_grp[g][:].bitcast(F32)[:, a * 2 * P:(a + 2) * 2 * P].rearrange("p (r q) -> p r q", q=2), u_ps[g, a][:].rearrange("p q r -> p r q"))
 
         def uq(g):
-            nc.vector.quantize_mx(out=u_codes[g][0][:].bitcast(FP8X4), scales=u_codes[g][1][:], in_=u_grp[g][:].rearrange("p m q -> p (m q)").bitcast(BF16))
+            v.quantize_mx(out=u_codes[g][0][:].bitcast(FP8X4), scales=u_codes[g][1][:], in_=u_grp[g][:])
 
-        s_ps = {}
+        s_ps, x, p_ps = {}, {}, {}
 
         def ts(j, q):
             for r in (RE, IM):
@@ -141,8 +148,6 @@ def tile_linearrecurrentunitcell_kernel(tc, inputs, state_re, state_im, B_re, B_
         def sview(j, t, r):
             return s_ps[j, t // 2, r][:].bitcast(BF16).rearrange("p (m e) -> p m e", e=2)[:, :, t % 2]
 
-        x = {}
-
         def a1(j, t):
             for r in (RE, IM):
                 if t == 0:
@@ -152,12 +157,10 @@ def tile_linearrecurrentunitcell_kernel(tc, inputs, state_re, state_im, B_re, B_
         def v2(j, t):
             for r, coef in ((RE, nli), (IM, li)):
                 xt = x[j, r][:, t, :]
-                nc.vector.scalar_tensor_tensor(out=xt, in0=sview(j, t, 1 - r), scalar=coef[:, t, j:j + 1], in1=xt, op0=Alu.mult, op1=Alu.add)
+                v.scalar_tensor_tensor(out=xt, in0=sview(j, t, 1 - r), scalar=coef[:, t, j:j + 1], in1=xt, op0=Alu.mult, op1=Alu.add)
 
-        p_ps = {}
-
-        def mm(j, t, rs=(RE, IM)):
-            for r in rs:
+        def mm(j, t):
+            for r in (RE, IM):
                 b = psum.tile([P, M], F32, tag=f"p{r}", name="p_ps")
                 for g in range(KP):
                     c, s = b_codes[j, r, g]
@@ -168,51 +171,68 @@ def tile_linearrecurrentunitcell_kernel(tc, inputs, state_re, state_im, B_re, B_
         def v3(j, t):
             for r in (RE, IM):
                 xt = x[j, r][:, t, :]
-                nc.vector.scalar_tensor_tensor(out=xt, in0=p_ps[j, t, r][:], scalar=ga[:, t, j:j + 1], in1=xt, op0=Alu.mult, op1=Alu.add)
+                v.scalar_tensor_tensor(out=xt, in0=p_ps[j, t, r][:], scalar=ga[:, t, j:j + 1], in1=xt, op0=Alu.mult, op1=Alu.add)
 
-        x_grp, x_codes = {}, {}
-        for j in range(BLOCKS):
-            for r in (RE, IM):
-                x_codes[j, r] = (keep.tile([P, M], U32, name=f"x_codes{j}{r}", align_bytes=64), keep.tile([P, M], U8, name=f"x_scales{j}{r}", align_bytes=64))
+        x_grp = {}
+        x_codes = {(j, r): (keep.tile([P, M], U32, name=f"x_codes{j}{r}", align_bytes=64), keep.tile([P, M], U8, name=f"x_scales{j}{r}", align_bytes=64)) for j in range(BLOCKS) for r in (RE, IM)}
 
         def cx(j, r):
-            t_ = ring.tile([P, HB * PACK], BF16, tag="grp", bufs=GRP, name="x_grp", align_bytes=64)
-            o = t_[:].rearrange("p (c n t) -> p c t n", n=4, t=PACK)
+            x_grp[j, r] = grp("x_grp")
+            o = x_grp[j, r][:].rearrange("p (c n t) -> p c t n", n=4, t=PACK)
             i = x[j, r][:].rearrange("p t (c n) -> p c t n", n=4)
             if r == RE:
-                nc.vector.tensor_copy(out=o, in_=i)
+                v.tensor_copy(out=o, in_=i)
             else:
-                nc.vector.tensor_scalar(out=o, in0=i, scalar1=-1.0, scalar2=None, op0=Alu.mult)
-            x_grp[j, r] = t_
+                v.tensor_scalar(out=o, in0=i, scalar1=-1.0, scalar2=None, op0=Alu.mult)
 
         def qx(j, r):
             c, s = x_codes[j, r]
-            nc.vector.quantize_mx(out=c[:].bitcast(FP8X4), scales=s[:], in_=x_grp[j, r][:])
-
-        o_n = [0]
+            v.quantize_mx(out=c[:].bitcast(FP8X4), scales=s[:], in_=x_grp[j, r][:])
 
         def to(j, r, a):
-            b = psum.tile([P, PACK, P], F32, tag=f"o{o_n[0] % 2}", name="o_ps")
-            o_n[0] += 1
+            b = psum.tile([P, PACK, P], F32, tag=f"o{a % 2}", name="o_ps")
             for t in range(PACK):
                 nc.tensor.transpose(b[:, t, :], x[j, r][:, t, a * P:(a + 1) * P], ident[:])
-            o = ring.tile([P, HB], F32, tag="o_sb", bufs=6, name="o_sb")
+            o = ring.tile([P, W], F32, tag="o_sb", bufs=OB, name="o_sb")
             nc.scalar.copy(o[:].rearrange("p (c t) -> p c t", t=PACK), b[:].rearrange("p t c -> p c t"))
-            nc.sync.dma_start(out=outs[r][a * P:(a + 1) * P, j * HB:(j + 1) * HB], in_=o[:])
+            nc.sync.dma_start(out=outs[r][a * P:(a + 1) * P, j * W:(j + 1) * W], in_=o[:])
 
-        load_b(0, RE, 0)
-        load_u(0)
-        load_u(2)
-        load_b(0, RE, 1)
-        load_b(0, IM, 0)
-        load_b(0, IM, 1)
-        load_s(0, RE)
-        load_s(0, IM)
-        for r in (RE, IM):
-            for g in range(KP):
-                load_b(1, r, g)
-        load_s(1, RE)
-        load_s(1, IM)
+        c_grp, c_codes = {}, {}
+
+        def widen(j, h):
+            w = ring.tile([P, PACK, W], BF16, tag="raw", bufs=RAW, name="c_w", align_bytes=64)
+            for t in range(PACK):
+                nc.scalar.activation(out=w[:, t, :], in_=c_raw[j, RE][:, t, h * W:(h + 1) * W].bitcast(FP8), func=Act.Copy, scale=cs_t[:, j, t:t + 1])
+            c_raw[j, "w", h] = w
+
+        def ci(eng, j, r, h):
+            c_grp[j, r, h] = grp("c_grp")
+            src = c_raw[j, "w", h][:] if r == RE else c_raw[j, IM][:, :, h * W:(h + 1) * W]
+            copy(eng, c_grp[j, r, h][:].rearrange("p (c n t) -> p c t n", n=4, t=PACK), src.rearrange("p t (c n) -> p c t n", n=4))
+
+        def cia(j, r, h):
+            ci("v" if (j, r, h) in VCI else "a", j, r, h)
+
+        def gci(k):
+            j, h, part = k // 4, k // 2 % 2, k % 2
+            if part == 0:
+                c_grp[j, IM, h] = grp("c_grp")
+            t_ = c_grp[j, IM, h][:, part * 1024:(part + 1) * 1024]
+            v.memset(t_[:, 0:2], 0.0)
+            src = c_raw[j, IM][:, :, h * W + part * 256:h * W + (part + 1) * 256]
+            return lambda: nc.gpsimd.tensor_scalar(out=t_.rearrange("p (n t) -> p n t", t=PACK), in0=src.rearrange("p t n -> p n t"), scalar1=1.0, scalar2=0.0, op0=Alu.mult, op1=Alu.add)
+
+        def cq(j, r, h):
+            if h == 0:
+                c_codes[j, r] = (ring.tile([P, N], U32, tag="c_codes", bufs=CC, name="c_codes", align_bytes=64), ring.tile([P, N], U8, tag="c_scales", bufs=CC, name="c_scales", align_bytes=64))
+            c, s = c_codes[j, r]
+            v.quantize_mx(out=c[:, h * W:(h + 1) * W].bitcast(FP8X4), scales=s[:, h * W:(h + 1) * W], in_=c_grp[j, r, h][:])
+
+        du = keep.tile([P, MT, N], F32, name="du")
+
+        def gdu(a):
+            v.memset(du[:, a, 0:1], 0.0)
+            return lambda: nc.gpsimd.tensor_tensor(out=du[:, a, :], in0=u_sb[:, a, :], in1=d_b[:], op=Alu.mult)
 
         def sm(name, dtype=F32):
             return keep.tile([P, PACK, BLOCKS], dtype, name=name)
@@ -221,20 +241,18 @@ def tile_linearrecurrentunitcell_kernel(tc, inputs, state_re, state_im, B_re, B_
             ("e1", "mag", "qi", "r1", "r2", "ab", "carg", "sh", "ch", "s2", "sc", "sc2", "lr", "li", "nli")]
         C1 = 6.28125
         C2 = 2.0 * math.pi - C1
-        v = nc.vector
         v_ps = psum.tile([P, PACK, P], BF16, tag="p0", name="v_ps")
         for t in range(PACK):
             nc.tensor.transpose(v_ps[:, t, :], lv[:, t::PACK], ident_b[:])
+        bi("v", 0, RE, 0)
         sv = keep.tile([P, PACK, 3 * BLOCKS], F32, name="sv")
         v.tensor_copy(out=sv[:], in_=v_ps[:, :, 0:3 * BLOCKS])
         th = sv[:, :, BLOCKS:2 * BLOCKS]
         ga = sv[:, :, 2 * BLOCKS:3 * BLOCKS]
         nc.scalar.activation(out=e1[:], in_=sv[:, :, 0:BLOCKS], func=Act.Exp)
         nc.scalar.activation(out=mag[:], in_=e1[:], func=Act.Exp, scale=-1.0)
+        bq(0, RE, 0)
         v.tensor_scalar(out=qi[:], in0=th, scalar1=1.0 / (2.0 * math.pi), scalar2=None, op0=Alu.mult)
-        v.scalar_tensor_tensor(out=r1[:], in0=qi[:], scalar=-C1, in1=th, op0=Alu.mult, op1=Alu.add)
-        bi("v", 0, RE, 0)
-        v.scalar_tensor_tensor(out=r2[:], in0=qi[:], scalar=-C2, in1=r1[:], op0=Alu.mult, op1=Alu.add)
         tu(0, 0, "s00")
         tu(1, 0, "s01")
         tu(0, 2, "s10")
@@ -243,99 +261,56 @@ def tile_linearrecurrentunitcell_kernel(tc, inputs, state_re, state_im, B_re, B_
         eu("a", 1, 0)
         eu("a", 0, 2)
         eu("a", 1, 2)
-        bq(0, RE, 0)
-        v.scalar_tensor_tensor(out=ab[:], in0=r2[:], scalar=-1.0, in1=r2[:], op0=Alu.mult, op1=Alu.max)
         bi("v", 0, RE, 1)
+        v.scalar_tensor_tensor(out=r1[:], in0=qi[:], scalar=-C1, in1=th, op0=Alu.mult, op1=Alu.add)
+        bq(0, RE, 1)
+        v.scalar_tensor_tensor(out=r2[:], in0=qi[:], scalar=-C2, in1=r1[:], op0=Alu.mult, op1=Alu.add)
+        uq(0)
+        v.scalar_tensor_tensor(out=ab[:], in0=r2[:], scalar=-1.0, in1=r2[:], op0=Alu.mult, op1=Alu.max)
+        uq(1)
         v.tensor_scalar(out=carg[:], in0=ab[:], scalar1=-0.5, scalar2=math.pi / 2.0, op0=Alu.mult, op1=Alu.add)
         nc.scalar.activation(out=sh[:], in_=r2[:], func=Act.Sin, scale=0.5)
         nc.scalar.activation(out=ch[:], in_=carg[:], func=Act.Sin)
-        uq(0)
-        bq(0, RE, 1)
-        uq(1)
         bi("a", 0, IM, 0)
         ts(0, 0)
+        bi("v", 0, IM, 1)
         v.tensor_tensor(out=s2[:], in0=sh[:], in1=sh[:], op=Alu.mult)
         v.scalar_tensor_tensor(out=sc[:], in0=sh[:], scalar=2.0, in1=ch[:], op0=Alu.mult, op1=Alu.mult)
         v.tensor_scalar(out=sc2[:], in0=s2[:], scalar1=-2.0, scalar2=1.0, op0=Alu.mult, op1=Alu.add)
         v.tensor_tensor(out=li[:], in0=sc[:], in1=mag[:], op=Alu.mult)
         v.tensor_tensor(out=lr[:], in0=sc2[:], in1=mag[:], op=Alu.mult)
-        bi("v", 0, IM, 1)
+        bq(0, IM, 0)
         v.tensor_scalar(out=nli[:], in0=li[:], scalar1=-1.0, scalar2=None, op0=Alu.mult)
         a1(0, 0)
-        bq(0, IM, 0)
         bq(0, IM, 1)
         ts(0, 1)
 
-        def widen(j, h):
-            w = ring.tile([P, PACK, 512], BF16, tag="raw", bufs=9, name="c_w", align_bytes=64)
-            for t in range(PACK):
-                nc.scalar.activation(out=w[:, t, :], in_=c_raw[j, RE][:, t, h * 512:(h + 1) * 512].bitcast(FP8), func=Act.Copy, scale=cs_t[:, j, t:t + 1])
-            c_raw[j, "w", h] = w
-
-        c_grp, c_codes = {}, {}
-
-        def ci(eng, j, r, h):
-            t_ = ring.tile([P, HB * PACK], BF16, tag="grp", bufs=GRP, name="c_grp", align_bytes=64)
-            src = c_raw[j, "w", h][:] if r == RE else c_raw[j, IM][:, :, h * 512:(h + 1) * 512]
-            o = t_[:].rearrange("p (c n t) -> p c t n", n=4, t=PACK)
-            i = src.rearrange("p t (c n) -> p c t n", n=4)
-            if eng == "v":
-                nc.vector.tensor_copy(out=o, in_=i)
-            else:
-                nc.scalar.copy(o, i)
-            c_grp[j, r, h] = t_
-
-        def cq(j, r, h):
-            if h == 0:
-                c_codes[j, r] = (ring.tile([P, N], U32, tag="c_codes", bufs=4, name="c_codes", align_bytes=64), ring.tile([P, N], U8, tag="c_scales", bufs=4, name="c_scales", align_bytes=64))
-            c, s = c_codes[j, r]
-            nc.vector.quantize_mx(out=c[:, h * 512:(h + 1) * 512].bitcast(FP8X4), scales=s[:, h * 512:(h + 1) * 512], in_=c_grp[j, r, h][:])
-
-        d_b = keep.tile([P, N], BF16, name="d_b")
-        nc.sync.dma_start(out=d_b[:], in_=D.partition_broadcast(P))
-        nc.sync.dma_start(out=cs_t[:], in_=C_re_scale.rearrange("(j p t) o -> p j (t o)", p=P, t=PACK))
-        du = keep.tile([P, MT, N], F32, name="du")
-
-        def dmul(k):
-            a, h = k // 2, k % 2
-            cols = slice(h * 512, (h + 1) * 512)
-            nc.vector.memset(du[:, a, h * 512:h * 512 + 1], 0.0)
-            return lambda: nc.gpsimd.tensor_tensor(out=du[:, a, cols], in0=u_sb[:, a, cols], in1=d_b[:, cols], op=Alu.mult)
-
-        y_tags = ["s00", "s01", "s10", "s11", "p0", "p1", "o0", "o1"]
-        banks = [(a, h) for h in range(2) for a in range(MT)]
-        y_ps = {}
-
-        def mm2(j, r, todo=None, first=False, last=False):
-            for b in (banks if todo is None else todo):
-                a, h = b
-                if first:
-                    y_ps[b] = psum.tile([P, 512], F32, tag=y_tags[banks.index(b)], name="y_ps")
-                xc, xs = x_codes[j, r]
-                c, s = c_codes[j, r]
-                nc.tensor.matmul_mx(out=y_ps[b][:], lhsT=xc[:, a * P:(a + 1) * P].bitcast(FP8X4), lhsT_scale=xs[:, a * P:(a + 1) * P],
-                                    rhs=c[:, h * 512:(h + 1) * 512].bitcast(FP8X4), rhs_scale=s[:, h * 512:(h + 1) * 512], start=first, stop=last)
-
-        PIECES = [(RE, 0), (RE, 1), (IM, 0), (IM, 1)]
-        L = BLOCKS - 1
+        gwork = {}
+        for a in range(MT):
+            gwork[(1 + a)] = lambda a=a: gdu(a)
+        for k in range(2 * GP):
+            gwork[5 + k] = lambda k=k: gci(k)
         for j in range(BLOCKS):
             nxt = j + 1 < BLOCKS
             prev = [(j - 1, r, a) for r in (RE, IM) for a in range(MT)] if j > 0 else []
             for t in range(PACK):
-                if j + 2 < BLOCKS:
-                    if t in (1, 3):
-                        for g in range(KP):
-                            load_b(j + 2, RE if t == 1 else IM, g)
-                        load_s(j + 2, RE if t == 1 else IM)
-                if j == 2:
-                    if t < 2:
-                        load_c(t, IM)
-                        load_c(t, RE)
+                if j + 2 < BLOCKS and t in (1, 3):
+                    for g in range(KP):
+                        load_b(j + 2, RE if t == 1 else IM, g)
+                    load_s(j + 2, RE if t == 1 else IM)
+                if (j, t) == (0, 2):
+                    load_cim(1)
+                    nc.sync.dma_start(out=cs_t[:], in_=C_re_scale.rearrange("(j p t) o -> p j (t o)", p=P, t=PACK))
+                if j == 2 and t in (0, 2):
+                    load_cre(t // 2)
+                if (j, t) == (2, 3):
+                    load_cim(2)
                 if t + 1 < PACK:
                     a1(j, t + 1)
-                g_ = dmul((j - 1) * PACK + t) if j in (1, 2) else (lambda: None)
+                g_ = gwork[4 * j + t]() if 4 * j + t in gwork else None
                 v2(j, t)
-                g_()
+                if g_:
+                    g_()
                 if t > 0:
                     v3(j, t - 1)
                 elif j > 0:
@@ -350,6 +325,10 @@ def tile_linearrecurrentunitcell_kernel(tc, inputs, state_re, state_im, B_re, B_
                     ts(j + 1, 0)
                 if t == 0 and j > 0:
                     ts(j, 1)
+                if not nxt and t == 0:
+                    widen(0, 0)
+                if nxt and t == 0:
+                    bi("v" if (j, t) in VBI else "a", j + 1, *PIECES[t])
                 for k in range(2):
                     if prev:
                         to(*prev.pop(0))
@@ -359,81 +338,91 @@ def tile_linearrecurrentunitcell_kernel(tc, inputs, state_re, state_im, B_re, B_
                     qx(j - 1, RE)
                 if t == 2 and j > 0:
                     qx(j - 1, IM)
+                k = 4 * j + t - 5
+                if k % 2 == 0 and 0 < k <= 2 * GP:
+                    cq((k - 2) // 4, IM, (k - 2) // 2 % 2)
                 if nxt:
-                    for part in range(2):
-                        bi("v" if (j, t, part) in VBI else "a", j + 1, *PIECES[t], part=part)
+                    if t > 0:
+                        bi("v" if (j, t) in VBI else "a", j + 1, *PIECES[t])
+                    if t == PACK - 1:
+                        a1(j + 1, 0)
                 else:
-                    if t < 2:
-                        widen(0, t)
+                    if t > 0:
+                        widen(t // 2, t % 2)
                     if t == 2:
-                        ci("v", 0, IM, 0)
-                        ci("a", 1, IM, 0)
+                        cia(0, RE, 0)
                     if t == 3:
-                        ci("v", 0, IM, 1)
-                        cq(0, IM, 0)
-                        ci("a", 1, IM, 1)
-                if t == PACK - 1 and nxt:
-                    a1(j + 1, 0)
+                        cia(0, RE, 1)
+                        cq(0, RE, 0)
 
-        load_c(2, IM)
-        load_c(2, RE)
+        y_tags = ["s00", "s01", "s10", "s11", "p0", "p1", "o0", "o1"]
+        banks = [(a, h) for h in range(2) for a in range(MT)]
+        y_ps = {}
+
+        def mm2(j, r, todo=None, first=False, last=False):
+            for b in (banks if todo is None else todo):
+                a, h = b
+                if first:
+                    y_ps[b] = psum.tile([P, W], F32, tag=y_tags[banks.index(b)], name="y_ps")
+                xc, xs = x_codes[j, r]
+                c, s = c_codes[j, r]
+                nc.tensor.matmul_mx(out=y_ps[b][:], lhsT=xc[:, a * P:(a + 1) * P].bitcast(FP8X4), lhsT_scale=xs[:, a * P:(a + 1) * P],
+                                    rhs=c[:, h * W:(h + 1) * W].bitcast(FP8X4), rhs_scale=s[:, h * W:(h + 1) * W], start=first, stop=last)
+
+        def ey(b):
+            a, h = b
+            y = ring.tile([P, W], F32, tag="o_sb", bufs=OB, name="y_sb")
+            v.tensor_tensor(out=y[:], in0=y_ps[b][:], in1=du[:, a, h * W:(h + 1) * W], op=Alu.add)
+            nc.sync.dma_start(out=out_0[a * P:(a + 1) * P, h * W:(h + 1) * W], in_=y[:])
+
+        L = BLOCKS - 1
+        load_cre(2)
+        load_cim(3)
         v3(L, PACK - 1)
-        cq(0, IM, 1)
-        ci("v", 0, RE, 0)
-        cq(1, IM, 0)
-        cx(L, RE)
-        cq(1, IM, 1)
-        to(L, RE, 0)
-        to(L, RE, 1)
-        widen(1, 0)
-        mm2(0, IM, banks[:6], True)
-        ci("v", 0, RE, 1)
-        cx(L, IM)
-        cq(0, RE, 0)
-        qx(L, RE)
-        to(L, RE, 2)
-        to(L, RE, 3)
-        widen(1, 1)
-        load_c(3, IM)
-        load_c(3, RE)
         cq(0, RE, 1)
+        cia(1, RE, 0)
+        cx(L, RE)
+        for a in range(MT):
+            to(L, RE, a)
+        cia(1, RE, 1)
+        cx(L, IM)
+        load_cre(3)
+        widen(2, 0)
+        cq(1, RE, 0)
+        qx(L, RE)
+        mm2(0, IM, banks[:6], True)
+        cq(1, RE, 1)
         qx(L, IM)
         for a in range(MT):
             to(L, IM, a)
+        widen(2, 1)
         mm2(0, IM, banks[6:], True)
         mm2(0, RE)
         mm2(1, IM)
-        ci("v", 1, RE, 0)
-        ci("v", 1, RE, 1)
-        widen(2, 0)
-        widen(2, 1)
-        ci("v", 2, IM, 0)
-        cq(1, RE, 0)
-        ci("v", 2, IM, 1)
-        cq(1, RE, 1)
+        cia(2, RE, 0)
+        cia(2, IM, 1)
         mm2(1, RE)
-        ci("a", 3, IM, 0)
-        widen(3, 0)
-        ci("v", 2, RE, 0)
-        cq(2, IM, 0)
-        ci("v", 2, RE, 1)
-        cq(2, IM, 1)
-        mm2(2, IM)
-        widen(3, 1)
-        ci("a", 3, IM, 1)
+        cia(2, RE, 1)
         cq(2, RE, 0)
-        ci("v", 3, RE, 0)
+        cq(2, IM, 1)
         cq(2, RE, 1)
+        mm2(2, IM)
+        widen(3, 0)
+        cia(3, IM, 0)
+        cia(3, RE, 0)
         mm2(2, RE)
-        ci("v" if LASTV else "a", 3, RE, 1)
+        widen(3, 1)
+        cia(3, IM, 1)
         cq(3, IM, 0)
         cq(3, RE, 0)
+        mm2(3, IM, banks[:MT])
+        mm2(3, RE, banks[:MT], last=True)
+        cia(3, RE, 1)
+        ey(banks[0])
+        ey(banks[1])
         cq(3, IM, 1)
-        mm2(3, IM)
         cq(3, RE, 1)
-        for n_, b in enumerate(banks):
-            a, h = b
-            mm2(3, RE, [b], False, True)
-            y = ring.tile([P, 512], F32, tag="o_sb", bufs=6, name="y_sb")
-            nc.vector.tensor_tensor(out=y[:], in0=y_ps[b][:], in1=du[:, a, h * 512:(h + 1) * 512], op=Alu.add)
-            nc.sync.dma_start(out=out_0[a * P:(a + 1) * P, h * 512:(h + 1) * 512], in_=y[:])
+        mm2(3, IM, banks[MT:])
+        mm2(3, RE, banks[MT:], last=True)
+        for b in banks[2:]:
+            ey(b)

@@ -21,408 +21,446 @@ P = 128
 PACK = 4
 W = P * PACK
 BLOCKS = H // W
-KP = N // W
+N_PASSES = N // W
 MT = M // P
+SLOTS = BLOCKS * PACK
 RE, IM = 0, 1
-RAW, GRP, BC, OB, CC = 8, 7, 7, 5, 5
-PIECES = [(RE, 0), (RE, 1), (IM, 0), (IM, 1)]
-VBI = {(0, 2), (1, 2), (2, 2)}
-GP = 5
-VCI = {(0, RE, 0), (0, RE, 1), (1, RE, 0), (1, RE, 1), (2, RE, 0), (2, RE, 1), (3, RE, 0), (3, RE, 1)}
+
+B_PIECES = [(RE, 0), (RE, 1), (IM, 0), (IM, 1)]
+VECTOR_B_SLOT = PACK - 1
+RUNS = 3
+RUNS_PER_HALF = W // P
+SKIP_SLOTS = range(4, 8)
+C_IM_SLOTS = range(8, SLOTS)
+SCALAR_C = {(RE, 2, 1), (IM, 3, 0)}
+C_IM_LOAD_SLOTS = [6, 8, 11, 14]
+C_RE_LOAD_SLOTS = [9, 10, 14]
+B_RAW_BUFS, GROUPED_BUFS, CODES_BUFS, STORE_BUFS = 8, 5, 7, 5
+
+TURN_HIGH = 6.28125
+TURN_LOW = 2.0 * math.pi - TURN_HIGH
 
 
 def tile_linearrecurrentunitcell_kernel(tc, inputs, state_re, state_im, B_re, B_im, C_re_bytes, C_re_scale, C_im, D, nu, theta, gamma, out_0, out_1, out_2):
     nc = tc.nc
-    states = (state_re, state_im)
-    Bs = (B_re, B_im)
-    outs = (out_1, out_2)
+    vec, act = nc.vector, nc.scalar
+    state = (state_re, state_im)
+    B = (B_re, B_im)
+    new_state_out = (out_1, out_2)
 
     with ExitStack() as ctx:
         keep = ctx.enter_context(tc.tile_pool(name="keep", bufs=1))
         ring = ctx.enter_context(tc.tile_pool(name="ring", bufs=2))
         psum = ctx.enter_context(tc.psum_pool(name="psum", bufs=1))
         ctx.enter_context(tc.manual_schedule())
-        v = nc.vector
 
-        lv = keep.tile([P, W], BF16, name="lv")
-        v.memset(lv[:], 0.0)
-        for n_, vec in enumerate((nu, theta, gamma)):
-            nc.sync.dma_start(out=lv[BLOCKS * n_:BLOCKS * (n_ + 1), :], in_=vec.rearrange("(j c) -> j c", j=BLOCKS))
+
+        vectors = keep.tile([P, W], BF16, name="vectors")
+        vec.memset(vectors[:], 0.0)
+        for i, vector in enumerate((nu, theta, gamma)):
+            nc.sync.dma_start(out=vectors[BLOCKS * i:BLOCKS * (i + 1), :], in_=vector.rearrange("(j c) -> j c", j=BLOCKS))
 
         b_raw, s_raw, c_raw = {}, {}, {}
 
         def load_b(j, r, g):
-            b_raw[j, r, g] = ring.tile([P, PACK, W], BF16, tag="raw", bufs=RAW, name="b_raw", align_bytes=64)
-            nc.sync.dma_start(out=b_raw[j, r, g][:], in_=Bs[r].rearrange("(g p i) h -> g p i h", p=P, i=PACK)[g][:, :, j * W:(j + 1) * W])
+            b_raw[j, r, g] = ring.tile([P, PACK, W], BF16, tag="raw", bufs=B_RAW_BUFS, name="b_raw", align_bytes=64)
+            nc.sync.dma_start(out=b_raw[j, r, g][:], in_=B[r].rearrange("(g p i) h -> g p i h", p=P, i=PACK)[g][:, :, j * W:(j + 1) * W])
 
-        def load_s(j, r):
+        def load_state(j, r):
             s_raw[j, r] = ring.tile([P, MT, W], BF16, tag="s_raw", bufs=4, name="s_raw", align_bytes=64)
-            nc.sync.dma_start(out=s_raw[j, r][:], in_=states[r].rearrange("(a p) h -> p a h", p=P)[:, :, j * W:(j + 1) * W])
+            nc.sync.dma_start(out=s_raw[j, r][:], in_=state[r].rearrange("(a p) h -> p a h", p=P)[:, :, j * W:(j + 1) * W])
 
-        u_sb = keep.tile([P, MT, N], BF16, name="u_sb", align_bytes=64)
+        u = keep.tile([P, MT, N], BF16, name="u", align_bytes=64)
 
-        def load_u(a):
-            nc.sync.dma_start(out=u_sb[:, a:a + 2, :], in_=inputs.rearrange("(a p) n -> p a n", p=P)[:, a:a + 2, :])
+        def load_inputs(a):
+            nc.sync.dma_start(out=u[:, a:a + 2, :], in_=inputs.rearrange("(a p) n -> p a n", p=P)[:, a:a + 2, :])
 
-        def load_cim(j):
-            c_raw[j, IM] = ring.tile([P, PACK, N], BF16, tag="cim_raw", bufs=2, name="cim_raw", align_bytes=64)
-            nc.sync.dma_start(out=c_raw[j, IM][:], in_=C_im.rearrange("(g p i) n -> g p i n", p=P, i=PACK)[j])
+        def load_c_im(j):
+            c_raw[IM, j] = ring.tile([P, PACK, N], BF16, tag="c_im_raw", bufs=2, name="c_im_raw", align_bytes=64)
+            nc.sync.dma_start(out=c_raw[IM, j][:], in_=C_im.rearrange("(g p i) n -> g p i n", p=P, i=PACK)[j])
 
-        def load_cre(j):
-            c_raw[j, RE] = ring.tile([P, PACK, N], U8, tag="cre_bytes", bufs=2, name="cre_bytes", align_bytes=64)
-            nc.sync.dma_start(out=c_raw[j, RE][:], in_=C_re_bytes.rearrange("(g p i) n -> g p i n", p=P, i=PACK)[j])
+        c_re_bytes = {}
 
-        d_b = keep.tile([P, N], BF16, name="d_b")
-        cs_t = keep.tile([P, BLOCKS, PACK], F32, name="cs_t")
+        def load_c_re(j):
+            c_re_bytes[j] = ring.tile([P, PACK, N], U8, tag="c_re_bytes", bufs=2, name="c_re_bytes", align_bytes=64)
+            nc.sync.dma_start(out=c_re_bytes[j][:], in_=C_re_bytes.rearrange("(g p i) n -> g p i n", p=P, i=PACK)[j])
+
+        d_all = keep.tile([P, N], BF16, name="d_all")
+        c_re_scale = keep.tile([P, BLOCKS, PACK], F32, name="c_re_scale")
 
         load_b(0, RE, 0)
-        load_u(0)
-        load_u(2)
+        load_inputs(0)
+        load_inputs(2)
         load_b(0, RE, 1)
         load_b(0, IM, 0)
         load_b(0, IM, 1)
-        load_s(0, RE)
-        load_s(0, IM)
-        nc.sync.dma_start(out=d_b[:], in_=D.partition_broadcast(P))
-        for r in (RE, IM):
-            for g in range(KP):
-                load_b(1, r, g)
-        load_s(1, RE)
-        load_s(1, IM)
-        load_cim(0)
+        load_state(0, RE)
+        load_state(0, IM)
+        for r, g in B_PIECES:
+            load_b(1, r, g)
+        load_state(1, RE)
+        load_state(1, IM)
 
         ident = keep.tile([P, P], F32, name="ident")
         make_identity(nc, ident[:])
-        ident_b = keep.tile([P, P], BF16, name="ident_b")
-        v.tensor_copy(out=ident_b[:], in_=ident[:])
+        ident_bf16 = keep.tile([P, P], BF16, name="ident_bf16")
+        vec.tensor_copy(out=ident_bf16[:], in_=ident[:])
 
-        def copy(eng, o, i):
-            if eng == "v":
-                v.tensor_copy(out=o, in_=i)
+
+        def copy(engine, out, in_):
+            if engine is vec:
+                vec.tensor_copy(out=out, in_=in_)
             else:
-                nc.scalar.copy(o, i)
+                act.copy(out, in_)
 
-        def grp(name):
-            return ring.tile([P, W * PACK], BF16, tag="grp", bufs=GRP, name=name, align_bytes=64)
+        def grouped_tile(name):
+            return ring.tile([P, W * PACK], BF16, tag="grouped", bufs=GROUPED_BUFS, name=name, align_bytes=64)
 
-        b_grp, b_codes = {}, {}
+        def codes_tiles(name):
+            return (ring.tile([P, W], U32, tag="codes", bufs=CODES_BUFS, name=name, align_bytes=64),
+                    ring.tile([P, W], U8, tag="scales", bufs=CODES_BUFS, name=name + "_scales", align_bytes=64))
 
-        def bi(eng, j, r, g):
-            b_grp[j, r, g] = grp("b_grp")
-            copy(eng, b_grp[j, r, g][:].rearrange("p (t m i) -> p m i t", t=PACK, i=PACK), b_raw[j, r, g][:].rearrange("p i (m t) -> p m i t", t=PACK))
+        def kept_codes_tiles(name):
+            return (keep.tile([P, W], U32, name=name, align_bytes=64), keep.tile([P, W], U8, name=name + "_scales", align_bytes=64))
 
-        def bq(j, r, g):
-            c = ring.tile([P, W], U32, tag="b_codes", bufs=BC, name="b_codes", align_bytes=64)
-            s = ring.tile([P, W], U8, tag="b_scales", bufs=BC, name="b_scales", align_bytes=64)
-            v.quantize_mx(out=c[:].bitcast(FP8X4), scales=s[:], in_=b_grp[j, r, g][:])
-            b_codes[j, r, g] = (c, s)
+        def quantise(codes, grouped):
+            vec.quantize_mx(out=codes[0][:].bitcast(FP8X4), scales=codes[1][:], in_=grouped[:])
 
-        u_grp = [grp("u_grp") for _ in range(KP)]
-        u_codes = [(keep.tile([P, M], U32, name=f"u_codes{g}", align_bytes=64), keep.tile([P, M], U8, name=f"u_scales{g}", align_bytes=64)) for g in range(KP)]
-        u_ps = {}
+        def matmul_mx(out, stationary, s0, moving, start, stop):
+            nc.tensor.matmul_mx(out=out, lhsT=stationary[0][:, s0:s0 + P].bitcast(FP8X4), lhsT_scale=stationary[1][:, s0:s0 + P],
+                                rhs=moving[0][:].bitcast(FP8X4), rhs_scale=moving[1][:], start=start, stop=stop)
 
-        def tu(g, a, bank):
-            b = psum.tile([P, 2, 256], F32, tag=bank, name="u_ps")
-            w = u_sb[:].bitcast(F32)
+        b_grouped, b_codes = {}, {}
+
+        def interleave_b(engine, j, r, g):
+            b_grouped[j, r, g] = grouped_tile("b_grouped")
+            copy(engine, b_grouped[j, r, g][:].rearrange("p (t m i) -> p m i t", t=PACK, i=PACK), b_raw[j, r, g][:].rearrange("p i (m t) -> p m i t", t=PACK))
+
+        def quantise_b(j, r, g):
+            b_codes[j, r, g] = codes_tiles("b_codes")
+            quantise(b_codes[j, r, g], b_grouped[j, r, g])
+
+        u_grouped = [grouped_tile(f"u_grouped{g}") for g in range(N_PASSES)]
+        u_codes = [kept_codes_tiles(f"u_codes{g}") for g in range(N_PASSES)]
+        u_banks = {}
+
+        def transpose_inputs(g, a, bank):
+            u_banks[g, a] = psum.tile([P, 2, 2 * P], F32, tag=bank, name="u_bank")
+            words = u[:].bitcast(F32)
             for i in range(2):
                 for q in range(2):
-                    nc.tensor.transpose(b[:, q, i * P:(i + 1) * P], w[:, a + i, 256 * g + q:256 * (g + 1):2], ident[:])
-            u_ps[g, a] = b
+                    nc.tensor.transpose(u_banks[g, a][:, q, i * P:(i + 1) * P], words[:, a + i, 256 * g + q:256 * (g + 1):2], ident[:])
 
-        def eu(eng, g, a):
-            copy(eng, u_grp[g][:].bitcast(F32)[:, a * 2 * P:(a + 2) * 2 * P].rearrange("p (r q) -> p r q", q=2), u_ps[g, a][:].rearrange("p q r -> p r q"))
+        def empty_inputs(g, a):
+            act.copy(u_grouped[g][:].bitcast(F32)[:, 2 * P * a:2 * P * (a + 2)].rearrange("p (r q) -> p r q", q=2), u_banks[g, a][:].rearrange("p q r -> p r q"))
 
-        def uq(g):
-            v.quantize_mx(out=u_codes[g][0][:].bitcast(FP8X4), scales=u_codes[g][1][:], in_=u_grp[g][:])
+        s_banks, x, u_b_banks = {}, {}, {}
 
-        s_ps, x, p_ps = {}, {}, {}
-
-        def ts(j, q):
+        def transpose_state(j, q):
             for r in (RE, IM):
-                b = psum.tile([P, M], F32, tag=f"s{q}{r}", name="s_ps")
-                w = s_raw[j, r][:].bitcast(F32)
+                s_banks[j, q, r] = psum.tile([P, M], F32, tag=f"s{q}{r}", name="s_bank")
+                words = s_raw[j, r][:].bitcast(F32)
                 for a in range(MT):
-                    nc.tensor.transpose(b[:, a * P:(a + 1) * P], w[:, a, q::2], ident[:])
-                s_ps[j, q, r] = b
+                    nc.tensor.transpose(s_banks[j, q, r][:, a * P:(a + 1) * P], words[:, a, q::2], ident[:])
 
-        def sview(j, t, r):
-            return s_ps[j, t // 2, r][:].bitcast(BF16).rearrange("p (m e) -> p m e", e=2)[:, :, t % 2]
+        def state_plane(j, t, r):
+            return s_banks[j, t // 2, r][:].bitcast(BF16).rearrange("p (m e) -> p m e", e=2)[:, :, t % 2]
 
-        def a1(j, t):
+        def scale_state(j, t):
             for r in (RE, IM):
                 if t == 0:
                     x[j, r] = ring.tile([P, PACK, M], F32, tag=f"x{r}", bufs=2, name="x", align_bytes=64)
-                nc.scalar.activation(out=x[j, r][:, t, :], in_=sview(j, t, r), func=Act.Copy, scale=lr[:, t, j:j + 1])
+                act.activation(out=x[j, r][:, t, :], in_=state_plane(j, t, r), func=Act.Copy, scale=lam_re[:, t, j:j + 1])
 
-        def v2(j, t):
-            for r, coef in ((RE, nli), (IM, li)):
-                xt = x[j, r][:, t, :]
-                v.scalar_tensor_tensor(out=xt, in0=sview(j, t, 1 - r), scalar=coef[:, t, j:j + 1], in1=xt, op0=Alu.mult, op1=Alu.add)
+        def add_cross_state(j, t):
+            for r, factor in ((RE, minus_lam_im), (IM, lam_im)):
+                plane = x[j, r][:, t, :]
+                vec.scalar_tensor_tensor(out=plane, in0=state_plane(j, t, 1 - r), scalar=factor[:, t, j:j + 1], in1=plane, op0=Alu.mult, op1=Alu.add)
 
-        def mm(j, t):
+        def multiply_inputs(j, t):
             for r in (RE, IM):
-                b = psum.tile([P, M], F32, tag=f"p{r}", name="p_ps")
-                for g in range(KP):
-                    c, s = b_codes[j, r, g]
-                    nc.tensor.matmul_mx(out=b[:], lhsT=c[:, t * P:(t + 1) * P].bitcast(FP8X4), lhsT_scale=s[:, t * P:(t + 1) * P],
-                                        rhs=u_codes[g][0][:].bitcast(FP8X4), rhs_scale=u_codes[g][1][:], start=(g == 0), stop=(g == KP - 1))
-                p_ps[j, t, r] = b
+                u_b_banks[j, t, r] = psum.tile([P, M], F32, tag=f"p{r}", name="u_b_bank")
+                for g in range(N_PASSES):
+                    matmul_mx(u_b_banks[j, t, r][:], b_codes[j, r, g], t * P, u_codes[g], g == 0, g == N_PASSES - 1)
 
-        def v3(j, t):
+        def add_inputs(j, t):
             for r in (RE, IM):
-                xt = x[j, r][:, t, :]
-                v.scalar_tensor_tensor(out=xt, in0=p_ps[j, t, r][:], scalar=ga[:, t, j:j + 1], in1=xt, op0=Alu.mult, op1=Alu.add)
+                plane = x[j, r][:, t, :]
+                vec.scalar_tensor_tensor(out=plane, in0=u_b_banks[j, t, r][:], scalar=gamma_col[:, t, j:j + 1], in1=plane, op0=Alu.mult, op1=Alu.add)
 
-        x_grp = {}
-        x_codes = {(j, r): (keep.tile([P, M], U32, name=f"x_codes{j}{r}", align_bytes=64), keep.tile([P, M], U8, name=f"x_scales{j}{r}", align_bytes=64)) for j in range(BLOCKS) for r in (RE, IM)}
+        x_grouped = {}
+        x_codes = {(j, r): kept_codes_tiles(f"x_codes{j}{r}") for j in range(BLOCKS) for r in (RE, IM)}
 
-        def cx(j, r):
-            x_grp[j, r] = grp("x_grp")
-            o = x_grp[j, r][:].rearrange("p (c n t) -> p c t n", n=4, t=PACK)
-            i = x[j, r][:].rearrange("p t (c n) -> p c t n", n=4)
+        def interleave_x(j, r):
+            x_grouped[j, r] = grouped_tile("x_grouped")
+            out = x_grouped[j, r][:].rearrange("p (c n t) -> p c t n", n=4, t=PACK)
+            in_ = x[j, r][:].rearrange("p t (c n) -> p c t n", n=4)
             if r == RE:
-                v.tensor_copy(out=o, in_=i)
+                vec.tensor_copy(out=out, in_=in_)
             else:
-                v.tensor_scalar(out=o, in0=i, scalar1=-1.0, scalar2=None, op0=Alu.mult)
+                vec.tensor_scalar(out=out, in0=in_, scalar1=-1.0, scalar2=None, op0=Alu.mult)
 
-        def qx(j, r):
-            c, s = x_codes[j, r]
-            v.quantize_mx(out=c[:].bitcast(FP8X4), scales=s[:], in_=x_grp[j, r][:])
+        def quantise_x(j, r):
+            quantise(x_codes[j, r], x_grouped[j, r])
 
-        def to(j, r, a):
-            b = psum.tile([P, PACK, P], F32, tag=f"o{a % 2}", name="o_ps")
+        def store_x(j, r, a):
+            bank = psum.tile([P, PACK, P], F32, tag=f"o{a % 2}", name="x_bank")
             for t in range(PACK):
-                nc.tensor.transpose(b[:, t, :], x[j, r][:, t, a * P:(a + 1) * P], ident[:])
-            o = ring.tile([P, W], F32, tag="o_sb", bufs=OB, name="o_sb")
-            nc.scalar.copy(o[:].rearrange("p (c t) -> p c t", t=PACK), b[:].rearrange("p t c -> p c t"))
-            nc.sync.dma_start(out=outs[r][a * P:(a + 1) * P, j * W:(j + 1) * W], in_=o[:])
+                nc.tensor.transpose(bank[:, t, :], x[j, r][:, t, a * P:(a + 1) * P], ident[:])
+            rows = ring.tile([P, W], F32, tag="rows", bufs=STORE_BUFS, name="x_rows")
+            act.copy(rows[:].rearrange("p (c t) -> p c t", t=PACK), bank[:].rearrange("p t c -> p c t"))
+            nc.sync.dma_start(out=new_state_out[r][a * P:(a + 1) * P, j * W:(j + 1) * W], in_=rows[:])
 
-        c_grp, c_codes = {}, {}
+        c_re_values, c_grouped, c_codes = {}, {}, {}
 
-        def widen(j, h):
-            w = ring.tile([P, PACK, W], BF16, tag="raw", bufs=RAW, name="c_w", align_bytes=64)
+        def widen_c_re(j, half):
+            c_re_values[j, half] = ring.tile([P, PACK, W], BF16, tag="raw", bufs=B_RAW_BUFS, name="c_re_values", align_bytes=64)
             for t in range(PACK):
-                nc.scalar.activation(out=w[:, t, :], in_=c_raw[j, RE][:, t, h * W:(h + 1) * W].bitcast(FP8), func=Act.Copy, scale=cs_t[:, j, t:t + 1])
-            c_raw[j, "w", h] = w
+                act.activation(out=c_re_values[j, half][:, t, :], in_=c_re_bytes[j][:, t, half * W:(half + 1) * W].bitcast(FP8), func=Act.Copy, scale=c_re_scale[:, j, t:t + 1])
 
-        def ci(eng, j, r, h):
-            c_grp[j, r, h] = grp("c_grp")
-            src = c_raw[j, "w", h][:] if r == RE else c_raw[j, IM][:, :, h * W:(h + 1) * W]
-            copy(eng, c_grp[j, r, h][:].rearrange("p (c n t) -> p c t n", n=4, t=PACK), src.rearrange("p t (c n) -> p c t n", n=4))
+        def interleave_c(r, j, half):
+            c_grouped[r, j, half] = grouped_tile("c_grouped")
+            rows = c_re_values[j, half][:] if r == RE else c_raw[IM, j][:, :, half * W:(half + 1) * W]
+            copy(act if (r, j, half) in SCALAR_C else vec, c_grouped[r, j, half][:].rearrange("p (c n t) -> p c t n", n=4, t=PACK), rows.rearrange("p t (c n) -> p c t n", n=4))
 
-        def cia(j, r, h):
-            ci("v" if (j, r, h) in VCI else "a", j, r, h)
+        def quantise_c(r, j, half):
+            c_codes[r, j, half] = kept_codes_tiles(f"c_im_codes{j}{half}") if r == IM else codes_tiles("c_re_codes")
+            quantise(c_codes[r, j, half], c_grouped[r, j, half])
 
-        def gci(k):
-            j, h, part = k // 4, k // 2 % 2, k % 2
-            if part == 0:
-                c_grp[j, IM, h] = grp("c_grp")
-            t_ = c_grp[j, IM, h][:, part * 1024:(part + 1) * 1024]
-            v.memset(t_[:, 0:2], 0.0)
-            src = c_raw[j, IM][:, :, h * W + part * 256:h * W + (part + 1) * 256]
-            return lambda: nc.gpsimd.tensor_scalar(out=t_.rearrange("p (n t) -> p n t", t=PACK), in0=src.rearrange("p t n -> p n t"), scalar1=1.0, scalar2=0.0, op0=Alu.mult, op1=Alu.add)
+        skip = keep.tile([P, MT, N], F32, name="skip")
 
-        def cq(j, r, h):
-            if h == 0:
-                c_codes[j, r] = (ring.tile([P, N], U32, tag="c_codes", bufs=CC, name="c_codes", align_bytes=64), ring.tile([P, N], U8, tag="c_scales", bufs=CC, name="c_scales", align_bytes=64))
-            c, s = c_codes[j, r]
-            v.quantize_mx(out=c[:, h * W:(h + 1) * W].bitcast(FP8X4), scales=s[:, h * W:(h + 1) * W], in_=c_grp[j, r, h][:])
 
-        du = keep.tile([P, MT, N], F32, name="du")
+        def gate_skip(a):
+            vec.memset(skip[:, a, 0:1], 0.0)
+            return lambda: nc.gpsimd.tensor_tensor(out=skip[:, a, :], in0=u[:, a, :], in1=d_all[:], op=Alu.mult)
 
-        def gdu(a):
-            v.memset(du[:, a, 0:1], 0.0)
-            return lambda: nc.gpsimd.tensor_tensor(out=du[:, a, :], in0=u_sb[:, a, :], in1=d_b[:], op=Alu.mult)
+        def gate_c_im(runs):
+            pieces = []
+            for run in runs:
+                j, half, first = run // (2 * RUNS_PER_HALF), run // RUNS_PER_HALF % 2, run % RUNS_PER_HALF
+                if first == 0:
+                    c_grouped[IM, j, half] = ring.tile([P, W * PACK], BF16, tag="c_im_grouped", bufs=3, name="c_im_grouped", align_bytes=64)
+                if pieces and pieces[-1][:2] == (j, half):
+                    pieces[-1] = (j, half, pieces[-1][2], first + 1)
+                else:
+                    pieces.append((j, half, first, first + 1))
+            j, half, first, end = pieces[0]
+            vec.memset(c_grouped[IM, j, half][:, first * W:first * W + 2], 0.0)
 
-        def sm(name, dtype=F32):
+            def issue():
+                for j, half, first, end in pieces:
+                    nc.gpsimd.tensor_scalar(out=c_grouped[IM, j, half][:, first * W:end * W].rearrange("p (n t) -> p n t", t=PACK),
+                                            in0=c_raw[IM, j][:, :, half * W + first * P:half * W + end * P].rearrange("p t n -> p n t"),
+                                            scalar1=1.0, scalar2=0.0, op0=Alu.mult, op1=Alu.add)
+            return issue
+
+        def gate(slot):
+            if slot in SKIP_SLOTS:
+                return gate_skip(slot - SKIP_SLOTS[0])
+            if slot in C_IM_SLOTS:
+                first = RUNS * (slot - C_IM_SLOTS[0])
+                return gate_c_im(range(first, first + RUNS))
+            return lambda: None
+
+        def c_im_halves_ready(slot):
+            done = RUNS * (slot - C_IM_SLOTS[0])
+            return [half for half in range(2 * BLOCKS) if max(done - RUNS, 0) < RUNS_PER_HALF * (half + 1) <= done]
+
+
+        def column(name, dtype=F32):
             return keep.tile([P, PACK, BLOCKS], dtype, name=name)
 
-        e1, mag, qi, r1, r2, ab, carg, sh, ch, s2, sc, sc2, lr, li, nli = [sm(n_, I32 if n_ == "qi" else F32) for n_ in
-            ("e1", "mag", "qi", "r1", "r2", "ab", "carg", "sh", "ch", "s2", "sc", "sc2", "lr", "li", "nli")]
-        C1 = 6.28125
-        C2 = 2.0 * math.pi - C1
-        v_ps = psum.tile([P, PACK, P], BF16, tag="p0", name="v_ps")
+        vectors_bank = psum.tile([P, PACK, P], BF16, tag="p0", name="vectors_bank")
         for t in range(PACK):
-            nc.tensor.transpose(v_ps[:, t, :], lv[:, t::PACK], ident_b[:])
-        bi("v", 0, RE, 0)
-        sv = keep.tile([P, PACK, 3 * BLOCKS], F32, name="sv")
-        v.tensor_copy(out=sv[:], in_=v_ps[:, :, 0:3 * BLOCKS])
-        th = sv[:, :, BLOCKS:2 * BLOCKS]
-        ga = sv[:, :, 2 * BLOCKS:3 * BLOCKS]
-        nc.scalar.activation(out=e1[:], in_=sv[:, :, 0:BLOCKS], func=Act.Exp)
-        nc.scalar.activation(out=mag[:], in_=e1[:], func=Act.Exp, scale=-1.0)
-        bq(0, RE, 0)
-        v.tensor_scalar(out=qi[:], in0=th, scalar1=1.0 / (2.0 * math.pi), scalar2=None, op0=Alu.mult)
-        tu(0, 0, "s00")
-        tu(1, 0, "s01")
-        tu(0, 2, "s10")
-        tu(1, 2, "s11")
-        eu("a", 0, 0)
-        eu("a", 1, 0)
-        eu("a", 0, 2)
-        eu("a", 1, 2)
-        bi("v", 0, RE, 1)
-        v.scalar_tensor_tensor(out=r1[:], in0=qi[:], scalar=-C1, in1=th, op0=Alu.mult, op1=Alu.add)
-        bq(0, RE, 1)
-        v.scalar_tensor_tensor(out=r2[:], in0=qi[:], scalar=-C2, in1=r1[:], op0=Alu.mult, op1=Alu.add)
-        uq(0)
-        v.scalar_tensor_tensor(out=ab[:], in0=r2[:], scalar=-1.0, in1=r2[:], op0=Alu.mult, op1=Alu.max)
-        uq(1)
-        v.tensor_scalar(out=carg[:], in0=ab[:], scalar1=-0.5, scalar2=math.pi / 2.0, op0=Alu.mult, op1=Alu.add)
-        nc.scalar.activation(out=sh[:], in_=r2[:], func=Act.Sin, scale=0.5)
-        nc.scalar.activation(out=ch[:], in_=carg[:], func=Act.Sin)
-        bi("a", 0, IM, 0)
-        ts(0, 0)
-        bi("v", 0, IM, 1)
-        v.tensor_tensor(out=s2[:], in0=sh[:], in1=sh[:], op=Alu.mult)
-        v.scalar_tensor_tensor(out=sc[:], in0=sh[:], scalar=2.0, in1=ch[:], op0=Alu.mult, op1=Alu.mult)
-        v.tensor_scalar(out=sc2[:], in0=s2[:], scalar1=-2.0, scalar2=1.0, op0=Alu.mult, op1=Alu.add)
-        v.tensor_tensor(out=li[:], in0=sc[:], in1=mag[:], op=Alu.mult)
-        v.tensor_tensor(out=lr[:], in0=sc2[:], in1=mag[:], op=Alu.mult)
-        bq(0, IM, 0)
-        v.tensor_scalar(out=nli[:], in0=li[:], scalar1=-1.0, scalar2=None, op0=Alu.mult)
-        a1(0, 0)
-        bq(0, IM, 1)
-        ts(0, 1)
+            nc.tensor.transpose(vectors_bank[:, t, :], vectors[:, t::PACK], ident_bf16[:])
+        interleave_b(vec, 0, RE, 0)
+        columns = keep.tile([P, PACK, 3 * BLOCKS], F32, name="columns")
+        vec.tensor_copy(out=columns[:], in_=vectors_bank[:, :, 0:3 * BLOCKS])
+        nu_col = columns[:, :, 0:BLOCKS]
+        theta_col = columns[:, :, BLOCKS:2 * BLOCKS]
+        gamma_col = columns[:, :, 2 * BLOCKS:3 * BLOCKS]
 
-        gwork = {}
-        for a in range(MT):
-            gwork[(1 + a)] = lambda a=a: gdu(a)
-        for k in range(2 * GP):
-            gwork[5 + k] = lambda k=k: gci(k)
+        exp_nu, magnitude = column("exp_nu"), column("magnitude")
+        act.activation(out=exp_nu[:], in_=nu_col, func=Act.Exp)
+        act.activation(out=magnitude[:], in_=exp_nu[:], func=Act.Exp, scale=-1.0)
+        quantise_b(0, RE, 0)
+
+        turns = column("turns", I32)
+        vec.tensor_scalar(out=turns[:], in0=theta_col, scalar1=1.0 / (2.0 * math.pi), scalar2=None, op0=Alu.mult)
+        transpose_inputs(0, 0, "s00")
+        transpose_inputs(1, 0, "s01")
+        transpose_inputs(0, 2, "s10")
+        transpose_inputs(1, 2, "s11")
+        empty_inputs(0, 0)
+        empty_inputs(1, 0)
+        empty_inputs(0, 2)
+        empty_inputs(1, 2)
+        interleave_b(vec, 0, RE, 1)
+        rough_angle, angle, abs_angle, complement = column("rough_angle"), column("angle"), column("abs_angle"), column("complement")
+        vec.scalar_tensor_tensor(out=rough_angle[:], in0=turns[:], scalar=-TURN_HIGH, in1=theta_col, op0=Alu.mult, op1=Alu.add)
+        quantise_b(0, RE, 1)
+        vec.scalar_tensor_tensor(out=angle[:], in0=turns[:], scalar=-TURN_LOW, in1=rough_angle[:], op0=Alu.mult, op1=Alu.add)
+        quantise(u_codes[0], u_grouped[0])
+        vec.scalar_tensor_tensor(out=abs_angle[:], in0=angle[:], scalar=-1.0, in1=angle[:], op0=Alu.mult, op1=Alu.max)
+        quantise(u_codes[1], u_grouped[1])
+        vec.tensor_scalar(out=complement[:], in0=abs_angle[:], scalar1=-0.5, scalar2=math.pi / 2.0, op0=Alu.mult, op1=Alu.add)
+        half_sin, half_cos = column("half_sin"), column("half_cos")
+        act.activation(out=half_sin[:], in_=angle[:], func=Act.Sin, scale=0.5)
+        act.activation(out=half_cos[:], in_=complement[:], func=Act.Sin)
+        interleave_b(act, 0, IM, 0)
+        transpose_state(0, 0)
+        interleave_b(vec, 0, IM, 1)
+        sin_squared, sin_theta, cos_theta = column("sin_squared"), column("sin_theta"), column("cos_theta")
+        lam_re, lam_im, minus_lam_im = column("lam_re"), column("lam_im"), column("minus_lam_im")
+        vec.tensor_tensor(out=sin_squared[:], in0=half_sin[:], in1=half_sin[:], op=Alu.mult)
+        vec.scalar_tensor_tensor(out=sin_theta[:], in0=half_sin[:], scalar=2.0, in1=half_cos[:], op0=Alu.mult, op1=Alu.mult)
+        vec.tensor_scalar(out=cos_theta[:], in0=sin_squared[:], scalar1=-2.0, scalar2=1.0, op0=Alu.mult, op1=Alu.add)
+        vec.tensor_tensor(out=lam_im[:], in0=sin_theta[:], in1=magnitude[:], op=Alu.mult)
+        vec.tensor_tensor(out=lam_re[:], in0=cos_theta[:], in1=magnitude[:], op=Alu.mult)
+        quantise_b(0, IM, 0)
+        vec.tensor_scalar(out=minus_lam_im[:], in0=lam_im[:], scalar1=-1.0, scalar2=None, op0=Alu.mult)
+        scale_state(0, 0)
+        quantise_b(0, IM, 1)
+        transpose_state(0, 1)
+
+
+        def vector_fillers(j, t):
+            slot = PACK * j + t
+            work = [lambda half=half: quantise_c(IM, half // 2, half % 2) for half in c_im_halves_ready(slot)]
+            if t == 0 and j > 0:
+                work.append(lambda: quantise_b(j, *B_PIECES[PACK - 1]))
+                work.append(lambda: interleave_x(j - 1, RE))
+            if t > 0 and j + 1 < BLOCKS:
+                work.append(lambda: quantise_b(j + 1, *B_PIECES[t - 1]))
+            if t == 1 and j > 0:
+                work.append(lambda: interleave_x(j - 1, IM))
+                work.append(lambda: quantise_x(j - 1, RE))
+            if t == 2 and j > 0:
+                work.append(lambda: quantise_x(j - 1, IM))
+            if t == VECTOR_B_SLOT and j + 1 < BLOCKS:
+                work.append(lambda: interleave_b(vec, j + 1, *B_PIECES[t]))
+            if slot == SLOTS - 2:
+                work.append(lambda: interleave_c(RE, 0, 0))
+            if slot == SLOTS - 1:
+                work.append(lambda: interleave_c(RE, 0, 1))
+                work.append(lambda: quantise_c(RE, 0, 0))
+            return work
+
         for j in range(BLOCKS):
-            nxt = j + 1 < BLOCKS
-            prev = [(j - 1, r, a) for r in (RE, IM) for a in range(MT)] if j > 0 else []
+            has_next = j + 1 < BLOCKS
+            to_store = [(j - 1, r, a) for r in (RE, IM) for a in range(MT)] if j > 0 else []
             for t in range(PACK):
-                if j + 2 < BLOCKS and t in (1, 3):
-                    for g in range(KP):
-                        load_b(j + 2, RE if t == 1 else IM, g)
-                    load_s(j + 2, RE if t == 1 else IM)
-                if (j, t) == (0, 2):
-                    load_cim(1)
-                    nc.sync.dma_start(out=cs_t[:], in_=C_re_scale.rearrange("(j p t) o -> p j (t o)", p=P, t=PACK))
-                if j == 2 and t in (0, 2):
-                    load_cre(t // 2)
-                if (j, t) == (2, 3):
-                    load_cim(2)
+                slot = PACK * j + t
+
+                if j + 2 < BLOCKS and t % 2 == 1:
+                    r = (RE, IM)[t // 2]
+                    for g in range(N_PASSES):
+                        load_b(j + 2, r, g)
+                    load_state(j + 2, r)
+                if slot == 2:
+                    nc.sync.dma_start(out=d_all[:], in_=D.partition_broadcast(P))
+                if slot == 3:
+                    nc.sync.dma_start(out=c_re_scale[:], in_=C_re_scale.rearrange("(j p t) o -> p j (t o)", p=P, t=PACK))
+                if slot in C_IM_LOAD_SLOTS:
+                    load_c_im(C_IM_LOAD_SLOTS.index(slot))
+                if slot in C_RE_LOAD_SLOTS:
+                    load_c_re(C_RE_LOAD_SLOTS.index(slot))
+
                 if t + 1 < PACK:
-                    a1(j, t + 1)
-                g_ = gwork[4 * j + t]() if 4 * j + t in gwork else None
-                v2(j, t)
-                if g_:
-                    g_()
-                if t > 0:
-                    v3(j, t - 1)
-                elif j > 0:
-                    v3(j - 1, PACK - 1)
-                if t == 0:
-                    if j > 0:
-                        bq(j, *PIECES[3])
-                        cx(j - 1, RE)
-                elif nxt:
-                    bq(j + 1, *PIECES[t - 1])
-                if t == 2 and nxt:
-                    ts(j + 1, 0)
-                if t == 0 and j > 0:
-                    ts(j, 1)
-                if not nxt and t == 0:
-                    widen(0, 0)
-                if nxt and t == 0:
-                    bi("v" if (j, t) in VBI else "a", j + 1, *PIECES[t])
-                for k in range(2):
-                    if prev:
-                        to(*prev.pop(0))
-                mm(j, t)
-                if t == 1 and j > 0:
-                    cx(j - 1, IM)
-                    qx(j - 1, RE)
-                if t == 2 and j > 0:
-                    qx(j - 1, IM)
-                k = 4 * j + t - 5
-                if k % 2 == 0 and 0 < k <= 2 * GP:
-                    cq((k - 2) // 4, IM, (k - 2) // 2 % 2)
-                if nxt:
-                    if t > 0:
-                        bi("v" if (j, t) in VBI else "a", j + 1, *PIECES[t])
-                    if t == PACK - 1:
-                        a1(j + 1, 0)
-                else:
-                    if t > 0:
-                        widen(t // 2, t % 2)
-                    if t == 2:
-                        cia(0, RE, 0)
-                    if t == 3:
-                        cia(0, RE, 1)
-                        cq(0, RE, 0)
+                    scale_state(j, t + 1)
+                add_cross_state(j, t)
+                if slot > 0:
+                    add_inputs((slot - 1) // PACK, (slot - 1) % PACK)
 
-        y_tags = ["s00", "s01", "s10", "s11", "p0", "p1", "o0", "o1"]
-        banks = [(a, h) for h in range(2) for a in range(MT)]
-        y_ps = {}
+                if t == 0 and has_next:
+                    interleave_b(act, j + 1, *B_PIECES[0])
+                if t == 0 and not has_next:
+                    widen_c_re(0, 0)
+                for store in to_store[2 * t:2 * t + 2]:
+                    store_x(*store)
+                if t > 0 and not has_next:
+                    widen_c_re(t // 2, t % 2)
 
-        def mm2(j, r, todo=None, first=False, last=False):
-            for b in (banks if todo is None else todo):
-                a, h = b
-                if first:
-                    y_ps[b] = psum.tile([P, W], F32, tag=y_tags[banks.index(b)], name="y_ps")
-                xc, xs = x_codes[j, r]
-                c, s = c_codes[j, r]
-                nc.tensor.matmul_mx(out=y_ps[b][:], lhsT=xc[:, a * P:(a + 1) * P].bitcast(FP8X4), lhsT_scale=xs[:, a * P:(a + 1) * P],
-                                    rhs=c[:, h * W:(h + 1) * W].bitcast(FP8X4), rhs_scale=s[:, h * W:(h + 1) * W], start=first, stop=last)
+                fillers = vector_fillers(j, t)
+                for work in fillers[:-1]:
+                    work()
+                issue_gpsimd = gate(slot + 1)
+                for work in fillers[-1:]:
+                    work()
+                issue_gpsimd()
 
-        def ey(b):
-            a, h = b
-            y = ring.tile([P, W], F32, tag="o_sb", bufs=OB, name="y_sb")
-            v.tensor_tensor(out=y[:], in0=y_ps[b][:], in1=du[:, a, h * W:(h + 1) * W], op=Alu.add)
-            nc.sync.dma_start(out=out_0[a * P:(a + 1) * P, h * W:(h + 1) * W], in_=y[:])
+                multiply_inputs(j, t)
+                if t % 2 == 1 and has_next:
+                    transpose_state(j + 1, t // 2)
+                if 0 < t < VECTOR_B_SLOT and has_next:
+                    interleave_b(act, j + 1, *B_PIECES[t])
+                if t == PACK - 1 and has_next:
+                    scale_state(j + 1, 0)
 
-        L = BLOCKS - 1
-        load_cre(2)
-        load_cim(3)
-        v3(L, PACK - 1)
-        cq(0, RE, 1)
-        cia(1, RE, 0)
-        cx(L, RE)
-        for a in range(MT):
-            to(L, RE, a)
-        cia(1, RE, 1)
-        cx(L, IM)
-        load_cre(3)
-        widen(2, 0)
-        cq(1, RE, 0)
-        qx(L, RE)
-        mm2(0, IM, banks[:6], True)
-        cq(1, RE, 1)
-        qx(L, IM)
-        for a in range(MT):
-            to(L, IM, a)
-        widen(2, 1)
-        mm2(0, IM, banks[6:], True)
-        mm2(0, RE)
-        mm2(1, IM)
-        cia(2, RE, 0)
-        cia(2, IM, 1)
-        mm2(1, RE)
-        cia(2, RE, 1)
-        cq(2, RE, 0)
-        cq(2, IM, 1)
-        cq(2, RE, 1)
-        mm2(2, IM)
-        widen(3, 0)
-        cia(3, IM, 0)
-        cia(3, RE, 0)
-        mm2(2, RE)
-        widen(3, 1)
-        cia(3, IM, 1)
-        cq(3, IM, 0)
-        cq(3, RE, 0)
-        mm2(3, IM, banks[:MT])
-        mm2(3, RE, banks[:MT], last=True)
-        cia(3, RE, 1)
-        ey(banks[0])
-        ey(banks[1])
-        cq(3, IM, 1)
-        cq(3, RE, 1)
-        mm2(3, IM, banks[MT:])
-        mm2(3, RE, banks[MT:], last=True)
-        for b in banks[2:]:
-            ey(b)
+
+        bank_tags = ["s00", "s01", "s10", "s11", "p0", "p1", "o0", "o1"]
+        banks = [(a, half) for half in range(2) for a in range(MT)]
+        early, late = banks[:6], banks[6:]
+        left, right = banks[:MT], banks[MT:]
+        y_banks = {}
+
+        def multiply_state(r, j, todo, start=False, stop=False):
+            for a, half in todo:
+                if start:
+                    y_banks[a, half] = psum.tile([P, W], F32, tag=bank_tags[banks.index((a, half))], name="y_bank")
+                matmul_mx(y_banks[a, half][:], x_codes[j, r], a * P, c_codes[r, j, half], start, stop)
+
+        def store_y(a, half):
+            rows = ring.tile([P, W], F32, tag="rows", bufs=STORE_BUFS, name="y_rows")
+            vec.tensor_tensor(out=rows[:], in0=y_banks[a, half][:], in1=skip[:, a, half * W:(half + 1) * W], op=Alu.add)
+            nc.sync.dma_start(out=out_0[a * P:(a + 1) * P, half * W:(half + 1) * W], in_=rows[:])
+
+        last = BLOCKS - 1
+        load_c_re(last)
+        add_inputs(last, PACK - 1)
+        widen_c_re(2, 0)
+        quantise_c(RE, 0, 1)
+        interleave_x(last, RE)
+        interleave_c(RE, 1, 0)
+        quantise_c(IM, 2, 1)
+        interleave_x(last, IM)
+        interleave_c(RE, 1, 1)
+
+        pairs = [(r, a) for r in (RE, IM) for a in (0, 2)]
+        for i, (r, a) in enumerate(pairs):
+            store_x(last, r, a)
+            store_x(last, r, a + 1)
+            if i == 1:
+                widen_c_re(2, 1)
+            if i < last:
+                multiply_state(IM, i, early, start=(i == 0))
+        quantise_x(last, RE)
+        quantise_c(RE, 1, 0)
+        quantise_x(last, IM)
+        quantise_c(RE, 1, 1)
+        for i in range(last):
+            multiply_state(IM, i, late, start=(i == 0))
+        multiply_state(RE, 0, banks)
+        multiply_state(RE, 1, banks)
+
+        interleave_c(RE, 2, 0)
+        interleave_c(RE, 2, 1)
+        widen_c_re(last, 0)
+        widen_c_re(last, 1)
+        interleave_c(IM, last, 1)
+        quantise_c(RE, 2, 0)
+        interleave_c(RE, last, 0)
+        quantise_c(RE, 2, 1)
+        multiply_state(RE, 2, banks)
+        interleave_c(IM, last, 0)
+        quantise_c(IM, last, 1)
+        quantise_c(RE, last, 0)
+        interleave_c(RE, last, 1)
+        quantise_c(IM, last, 0)
+        multiply_state(RE, last, left)
+        multiply_state(IM, last, left, stop=True)
+        quantise_c(RE, last, 1)
+        multiply_state(IM, last, right)
+        multiply_state(RE, last, right, stop=True)
+        for a, half in banks:
+            store_y(a, half)

import math
from contextlib import ExitStack

import concourse.mybir as mybir
from concourse.masks import make_identity

M, N, H = 512, 1024, 2048
FLOPS = 8 * M * N * H

F32 = mybir.dt.float32
BF16 = mybir.dt.bfloat16
U32 = mybir.dt.uint32
I32 = mybir.dt.int32
U8 = mybir.dt.uint8
FP8 = mybir.dt.float8_e4m3fn
FP8X4 = mybir.dt.float8_e4m3fn_x4
Act = mybir.ActivationFunctionType
Alu = mybir.AluOpType

P = 128
PACK = 4
W = P * PACK
BLOCKS = H // W
N_PASSES = N // W
MT = M // P
SLOTS = BLOCKS * PACK
RE, IM = 0, 1

B_PIECES = [(RE, 0), (RE, 1), (IM, 0), (IM, 1)]
VECTOR_B_SLOT = PACK - 1
RUNS = 3
RUNS_PER_HALF = W // P
SKIP_SLOTS = range(4, 8)
C_IM_SLOTS = range(8, SLOTS)
SCALAR_C = {(RE, 2, 1), (IM, 3, 0)}
C_IM_LOAD_SLOTS = [6, 8, 11, 14]
C_RE_LOAD_SLOTS = [9, 10, 14]
B_RAW_BUFS, GROUPED_BUFS, CODES_BUFS, STORE_BUFS = 8, 5, 7, 5

TURN_HIGH = 6.28125
TURN_LOW = 2.0 * math.pi - TURN_HIGH


def tile_linearrecurrentunitcell_kernel(tc, inputs, state_re, state_im, B_re, B_im, C_re_bytes, C_re_scale, C_im, D, nu, theta, gamma, out_0, out_1, out_2):
    nc = tc.nc
    vec, act = nc.vector, nc.scalar
    state = (state_re, state_im)
    B = (B_re, B_im)
    new_state_out = (out_1, out_2)

    with ExitStack() as ctx:
        keep = ctx.enter_context(tc.tile_pool(name="keep", bufs=1))
        ring = ctx.enter_context(tc.tile_pool(name="ring", bufs=2))
        psum = ctx.enter_context(tc.psum_pool(name="psum", bufs=1))
        ctx.enter_context(tc.manual_schedule())


        vectors = keep.tile([P, W], BF16, name="vectors")
        vec.memset(vectors[:], 0.0)
        for i, vector in enumerate((nu, theta, gamma)):
            nc.sync.dma_start(out=vectors[BLOCKS * i:BLOCKS * (i + 1), :], in_=vector.rearrange("(j c) -> j c", j=BLOCKS))

        b_raw, s_raw, c_raw = {}, {}, {}

        def load_b(j, r, g):
            b_raw[j, r, g] = ring.tile([P, PACK, W], BF16, tag="raw", bufs=B_RAW_BUFS, name="b_raw", align_bytes=64)
            nc.sync.dma_start(out=b_raw[j, r, g][:], in_=B[r].rearrange("(g p i) h -> g p i h", p=P, i=PACK)[g][:, :, j * W:(j + 1) * W])

        def load_state(j, r):
            s_raw[j, r] = ring.tile([P, MT, W], BF16, tag="s_raw", bufs=4, name="s_raw", align_bytes=64)
            nc.sync.dma_start(out=s_raw[j, r][:], in_=state[r].rearrange("(a p) h -> p a h", p=P)[:, :, j * W:(j + 1) * W])

        u = keep.tile([P, MT, N], BF16, name="u", align_bytes=64)

        def load_inputs(a):
            nc.sync.dma_start(out=u[:, a:a + 2, :], in_=inputs.rearrange("(a p) n -> p a n", p=P)[:, a:a + 2, :])

        def load_c_im(j):
            c_raw[IM, j] = ring.tile([P, PACK, N], BF16, tag="c_im_raw", bufs=2, name="c_im_raw", align_bytes=64)
            nc.sync.dma_start(out=c_raw[IM, j][:], in_=C_im.rearrange("(g p i) n -> g p i n", p=P, i=PACK)[j])

        c_re_bytes = {}

        def load_c_re(j):
            c_re_bytes[j] = ring.tile([P, PACK, N], U8, tag="c_re_bytes", bufs=2, name="c_re_bytes", align_bytes=64)
            nc.sync.dma_start(out=c_re_bytes[j][:], in_=C_re_bytes.rearrange("(g p i) n -> g p i n", p=P, i=PACK)[j])

        d_all = keep.tile([P, N], BF16, name="d_all")
        c_re_scale = keep.tile([P, BLOCKS, PACK], F32, name="c_re_scale")

        load_b(0, RE, 0)
        load_inputs(0)
        load_inputs(2)
        load_b(0, RE, 1)
        load_b(0, IM, 0)
        load_b(0, IM, 1)
        load_state(0, RE)
        load_state(0, IM)
        for r, g in B_PIECES:
            load_b(1, r, g)
        load_state(1, RE)
        load_state(1, IM)

        ident = keep.tile([P, P], F32, name="ident")
        make_identity(nc, ident[:])
        ident_bf16 = keep.tile([P, P], BF16, name="ident_bf16")
        vec.tensor_copy(out=ident_bf16[:], in_=ident[:])


        def copy(engine, out, in_):
            if engine is vec:
                vec.tensor_copy(out=out, in_=in_)
            else:
                act.copy(out, in_)

        def grouped_tile(name):
            return ring.tile([P, W * PACK], BF16, tag="grouped", bufs=GROUPED_BUFS, name=name, align_bytes=64)

        def codes_tiles(name):
            return (ring.tile([P, W], U32, tag="codes", bufs=CODES_BUFS, name=name, align_bytes=64),
                    ring.tile([P, W], U8, tag="scales", bufs=CODES_BUFS, name=name + "_scales", align_bytes=64))

        def kept_codes_tiles(name):
            return (keep.tile([P, W], U32, name=name, align_bytes=64), keep.tile([P, W], U8, name=name + "_scales", align_bytes=64))

        def quantise(codes, grouped):
            vec.quantize_mx(out=codes[0][:].bitcast(FP8X4), scales=codes[1][:], in_=grouped[:])

        def matmul_mx(out, stationary, s0, moving, start, stop):
            nc.tensor.matmul_mx(out=out, lhsT=stationary[0][:, s0:s0 + P].bitcast(FP8X4), lhsT_scale=stationary[1][:, s0:s0 + P],
                                rhs=moving[0][:].bitcast(FP8X4), rhs_scale=moving[1][:], start=start, stop=stop)

        b_grouped, b_codes = {}, {}

        def interleave_b(engine, j, r, g):
            b_grouped[j, r, g] = grouped_tile("b_grouped")
            copy(engine, b_grouped[j, r, g][:].rearrange("p (t m i) -> p m i t", t=PACK, i=PACK), b_raw[j, r, g][:].rearrange("p i (m t) -> p m i t", t=PACK))

        def quantise_b(j, r, g):
            b_codes[j, r, g] = codes_tiles("b_codes")
            quantise(b_codes[j, r, g], b_grouped[j, r, g])

        u_grouped = [grouped_tile(f"u_grouped{g}") for g in range(N_PASSES)]
        u_codes = [kept_codes_tiles(f"u_codes{g}") for g in range(N_PASSES)]
        u_banks = {}

        def transpose_inputs(g, a, bank):
            u_banks[g, a] = psum.tile([P, 2, 2 * P], F32, tag=bank, name="u_bank")
            words = u[:].bitcast(F32)
            for i in range(2):
                for q in range(2):
                    nc.tensor.transpose(u_banks[g, a][:, q, i * P:(i + 1) * P], words[:, a + i, 256 * g + q:256 * (g + 1):2], ident[:])

        def empty_inputs(g, a):
            act.copy(u_grouped[g][:].bitcast(F32)[:, 2 * P * a:2 * P * (a + 2)].rearrange("p (r q) -> p r q", q=2), u_banks[g, a][:].rearrange("p q r -> p r q"))

        s_banks, x, u_b_banks = {}, {}, {}

        def transpose_state(j, q):
            for r in (RE, IM):
                s_banks[j, q, r] = psum.tile([P, M], F32, tag=f"s{q}{r}", name="s_bank")
                words = s_raw[j, r][:].bitcast(F32)
                for a in range(MT):
                    nc.tensor.transpose(s_banks[j, q, r][:, a * P:(a + 1) * P], words[:, a, q::2], ident[:])

        def state_plane(j, t, r):
            return s_banks[j, t // 2, r][:].bitcast(BF16).rearrange("p (m e) -> p m e", e=2)[:, :, t % 2]

        def scale_state(j, t):
            for r in (RE, IM):
                if t == 0:
                    x[j, r] = ring.tile([P, PACK, M], F32, tag=f"x{r}", bufs=2, name="x", align_bytes=64)
                act.activation(out=x[j, r][:, t, :], in_=state_plane(j, t, r), func=Act.Copy, scale=lam_re[:, t, j:j + 1])

        def add_cross_state(j, t):
            for r, factor in ((RE, minus_lam_im), (IM, lam_im)):
                plane = x[j, r][:, t, :]
                vec.scalar_tensor_tensor(out=plane, in0=state_plane(j, t, 1 - r), scalar=factor[:, t, j:j + 1], in1=plane, op0=Alu.mult, op1=Alu.add)

        def multiply_inputs(j, t):
            for r in (RE, IM):
                u_b_banks[j, t, r] = psum.tile([P, M], F32, tag=f"p{r}", name="u_b_bank")
                for g in range(N_PASSES):
                    matmul_mx(u_b_banks[j, t, r][:], b_codes[j, r, g], t * P, u_codes[g], g == 0, g == N_PASSES - 1)

        def add_inputs(j, t):
            for r in (RE, IM):
                plane = x[j, r][:, t, :]
                vec.scalar_tensor_tensor(out=plane, in0=u_b_banks[j, t, r][:], scalar=gamma_col[:, t, j:j + 1], in1=plane, op0=Alu.mult, op1=Alu.add)

        x_grouped = {}
        x_codes = {(j, r): kept_codes_tiles(f"x_codes{j}{r}") for j in range(BLOCKS) for r in (RE, IM)}

        def interleave_x(j, r):
            x_grouped[j, r] = grouped_tile("x_grouped")
            out = x_grouped[j, r][:].rearrange("p (c n t) -> p c t n", n=4, t=PACK)
            in_ = x[j, r][:].rearrange("p t (c n) -> p c t n", n=4)
            if r == RE:
                vec.tensor_copy(out=out, in_=in_)
            else:
                vec.tensor_scalar(out=out, in0=in_, scalar1=-1.0, scalar2=None, op0=Alu.mult)

        def quantise_x(j, r):
            quantise(x_codes[j, r], x_grouped[j, r])

        def store_x(j, r, a):
            bank = psum.tile([P, PACK, P], F32, tag=f"o{a % 2}", name="x_bank")
            for t in range(PACK):
                nc.tensor.transpose(bank[:, t, :], x[j, r][:, t, a * P:(a + 1) * P], ident[:])
            rows = ring.tile([P, W], F32, tag="rows", bufs=STORE_BUFS, name="x_rows")
            act.copy(rows[:].rearrange("p (c t) -> p c t", t=PACK), bank[:].rearrange("p t c -> p c t"))
            nc.sync.dma_start(out=new_state_out[r][a * P:(a + 1) * P, j * W:(j + 1) * W], in_=rows[:])

        c_re_values, c_grouped, c_codes = {}, {}, {}

        def widen_c_re(j, half):
            c_re_values[j, half] = ring.tile([P, PACK, W], BF16, tag="raw", bufs=B_RAW_BUFS, name="c_re_values", align_bytes=64)
            for t in range(PACK):
                act.activation(out=c_re_values[j, half][:, t, :], in_=c_re_bytes[j][:, t, half * W:(half + 1) * W].bitcast(FP8), func=Act.Copy, scale=c_re_scale[:, j, t:t + 1])

        def interleave_c(r, j, half):
            c_grouped[r, j, half] = grouped_tile("c_grouped")
            rows = c_re_values[j, half][:] if r == RE else c_raw[IM, j][:, :, half * W:(half + 1) * W]
            copy(act if (r, j, half) in SCALAR_C else vec, c_grouped[r, j, half][:].rearrange("p (c n t) -> p c t n", n=4, t=PACK), rows.rearrange("p t (c n) -> p c t n", n=4))

        def quantise_c(r, j, half):
            c_codes[r, j, half] = kept_codes_tiles(f"c_im_codes{j}{half}") if r == IM else codes_tiles("c_re_codes")
            quantise(c_codes[r, j, half], c_grouped[r, j, half])

        skip = keep.tile([P, MT, N], F32, name="skip")


        def gate_skip(a):
            vec.memset(skip[:, a, 0:1], 0.0)
            return lambda: nc.gpsimd.tensor_tensor(out=skip[:, a, :], in0=u[:, a, :], in1=d_all[:], op=Alu.mult)

        def gate_c_im(runs):
            pieces = []
            for run in runs:
                j, half, first = run // (2 * RUNS_PER_HALF), run // RUNS_PER_HALF % 2, run % RUNS_PER_HALF
                if first == 0:
                    c_grouped[IM, j, half] = ring.tile([P, W * PACK], BF16, tag="c_im_grouped", bufs=3, name="c_im_grouped", align_bytes=64)
                if pieces and pieces[-1][:2] == (j, half):
                    pieces[-1] = (j, half, pieces[-1][2], first + 1)
                else:
                    pieces.append((j, half, first, first + 1))
            j, half, first, end = pieces[0]
            vec.memset(c_grouped[IM, j, half][:, first * W:first * W + 2], 0.0)

            def issue():
                for j, half, first, end in pieces:
                    nc.gpsimd.tensor_scalar(out=c_grouped[IM, j, half][:, first * W:end * W].rearrange("p (n t) -> p n t", t=PACK),
                                            in0=c_raw[IM, j][:, :, half * W + first * P:half * W + end * P].rearrange("p t n -> p n t"),
                                            scalar1=1.0, scalar2=0.0, op0=Alu.mult, op1=Alu.add)
            return issue

        def gate(slot):
            if slot in SKIP_SLOTS:
                return gate_skip(slot - SKIP_SLOTS[0])
            if slot in C_IM_SLOTS:
                first = RUNS * (slot - C_IM_SLOTS[0])
                return gate_c_im(range(first, first + RUNS))
            return lambda: None

        def c_im_halves_ready(slot):
            done = RUNS * (slot - C_IM_SLOTS[0])
            return [half for half in range(2 * BLOCKS) if max(done - RUNS, 0) < RUNS_PER_HALF * (half + 1) <= done]


        def column(name, dtype=F32):
            return keep.tile([P, PACK, BLOCKS], dtype, name=name)

        vectors_bank = psum.tile([P, PACK, P], BF16, tag="p0", name="vectors_bank")
        for t in range(PACK):
            nc.tensor.transpose(vectors_bank[:, t, :], vectors[:, t::PACK], ident_bf16[:])
        interleave_b(vec, 0, RE, 0)
        columns = keep.tile([P, PACK, 3 * BLOCKS], F32, name="columns")
        vec.tensor_copy(out=columns[:], in_=vectors_bank[:, :, 0:3 * BLOCKS])
        nu_col = columns[:, :, 0:BLOCKS]
        theta_col = columns[:, :, BLOCKS:2 * BLOCKS]
        gamma_col = columns[:, :, 2 * BLOCKS:3 * BLOCKS]

        exp_nu, magnitude = column("exp_nu"), column("magnitude")
        act.activation(out=exp_nu[:], in_=nu_col, func=Act.Exp)
        act.activation(out=magnitude[:], in_=exp_nu[:], func=Act.Exp, scale=-1.0)
        quantise_b(0, RE, 0)

        turns = column("turns", I32)
        vec.tensor_scalar(out=turns[:], in0=theta_col, scalar1=1.0 / (2.0 * math.pi), scalar2=None, op0=Alu.mult)
        transpose_inputs(0, 0, "s00")
        transpose_inputs(1, 0, "s01")
        transpose_inputs(0, 2, "s10")
        transpose_inputs(1, 2, "s11")
        empty_inputs(0, 0)
        empty_inputs(1, 0)
        empty_inputs(0, 2)
        empty_inputs(1, 2)
        interleave_b(vec, 0, RE, 1)
        rough_angle, angle, abs_angle, complement = column("rough_angle"), column("angle"), column("abs_angle"), column("complement")
        vec.scalar_tensor_tensor(out=rough_angle[:], in0=turns[:], scalar=-TURN_HIGH, in1=theta_col, op0=Alu.mult, op1=Alu.add)
        quantise_b(0, RE, 1)
        vec.scalar_tensor_tensor(out=angle[:], in0=turns[:], scalar=-TURN_LOW, in1=rough_angle[:], op0=Alu.mult, op1=Alu.add)
        quantise(u_codes[0], u_grouped[0])
        vec.scalar_tensor_tensor(out=abs_angle[:], in0=angle[:], scalar=-1.0, in1=angle[:], op0=Alu.mult, op1=Alu.max)
        quantise(u_codes[1], u_grouped[1])
        vec.tensor_scalar(out=complement[:], in0=abs_angle[:], scalar1=-0.5, scalar2=math.pi / 2.0, op0=Alu.mult, op1=Alu.add)
        half_sin, half_cos = column("half_sin"), column("half_cos")
        act.activation(out=half_sin[:], in_=angle[:], func=Act.Sin, scale=0.5)
        act.activation(out=half_cos[:], in_=complement[:], func=Act.Sin)
        interleave_b(act, 0, IM, 0)
        transpose_state(0, 0)
        interleave_b(vec, 0, IM, 1)
        sin_squared, sin_theta, cos_theta = column("sin_squared"), column("sin_theta"), column("cos_theta")
        lam_re, lam_im, minus_lam_im = column("lam_re"), column("lam_im"), column("minus_lam_im")
        vec.tensor_tensor(out=sin_squared[:], in0=half_sin[:], in1=half_sin[:], op=Alu.mult)
        vec.scalar_tensor_tensor(out=sin_theta[:], in0=half_sin[:], scalar=2.0, in1=half_cos[:], op0=Alu.mult, op1=Alu.mult)
        vec.tensor_scalar(out=cos_theta[:], in0=sin_squared[:], scalar1=-2.0, scalar2=1.0, op0=Alu.mult, op1=Alu.add)
        vec.tensor_tensor(out=lam_im[:], in0=sin_theta[:], in1=magnitude[:], op=Alu.mult)
        vec.tensor_tensor(out=lam_re[:], in0=cos_theta[:], in1=magnitude[:], op=Alu.mult)
        quantise_b(0, IM, 0)
        vec.tensor_scalar(out=minus_lam_im[:], in0=lam_im[:], scalar1=-1.0, scalar2=None, op0=Alu.mult)
        scale_state(0, 0)
        quantise_b(0, IM, 1)
        transpose_state(0, 1)


        def vector_fillers(j, t):
            slot = PACK * j + t
            work = [lambda half=half: quantise_c(IM, half // 2, half % 2) for half in c_im_halves_ready(slot)]
            if t == 0 and j > 0:
                work.append(lambda: quantise_b(j, *B_PIECES[PACK - 1]))
                work.append(lambda: interleave_x(j - 1, RE))
            if t > 0 and j + 1 < BLOCKS:
                work.append(lambda: quantise_b(j + 1, *B_PIECES[t - 1]))
            if t == 1 and j > 0:
                work.append(lambda: interleave_x(j - 1, IM))
                work.append(lambda: quantise_x(j - 1, RE))
            if t == 2 and j > 0:
                work.append(lambda: quantise_x(j - 1, IM))
            if t == VECTOR_B_SLOT and j + 1 < BLOCKS:
                work.append(lambda: interleave_b(vec, j + 1, *B_PIECES[t]))
            if slot == SLOTS - 2:
                work.append(lambda: interleave_c(RE, 0, 0))
            if slot == SLOTS - 1:
                work.append(lambda: interleave_c(RE, 0, 1))
                work.append(lambda: quantise_c(RE, 0, 0))
            return work

        for j in range(BLOCKS):
            has_next = j + 1 < BLOCKS
            to_store = [(j - 1, r, a) for r in (RE, IM) for a in range(MT)] if j > 0 else []
            for t in range(PACK):
                slot = PACK * j + t

                if j + 2 < BLOCKS and t % 2 == 1:
                    r = (RE, IM)[t // 2]
                    for g in range(N_PASSES):
                        load_b(j + 2, r, g)
                    load_state(j + 2, r)
                if slot == 2:
                    nc.sync.dma_start(out=d_all[:], in_=D.partition_broadcast(P))
                if slot == 3:
                    nc.sync.dma_start(out=c_re_scale[:], in_=C_re_scale.rearrange("(j p t) o -> p j (t o)", p=P, t=PACK))
                if slot in C_IM_LOAD_SLOTS:
                    load_c_im(C_IM_LOAD_SLOTS.index(slot))
                if slot in C_RE_LOAD_SLOTS:
                    load_c_re(C_RE_LOAD_SLOTS.index(slot))

                if t + 1 < PACK:
                    scale_state(j, t + 1)
                add_cross_state(j, t)
                if slot > 0:
                    add_inputs((slot - 1) // PACK, (slot - 1) % PACK)

                if t == 0 and has_next:
                    interleave_b(act, j + 1, *B_PIECES[0])
                if t == 0 and not has_next:
                    widen_c_re(0, 0)
                for store in to_store[2 * t:2 * t + 2]:
                    store_x(*store)
                if t > 0 and not has_next:
                    widen_c_re(t // 2, t % 2)

                fillers = vector_fillers(j, t)
                for work in fillers[:-1]:
                    work()
                issue_gpsimd = gate(slot + 1)
                for work in fillers[-1:]:
                    work()
                issue_gpsimd()

                multiply_inputs(j, t)
                if t % 2 == 1 and has_next:
                    transpose_state(j + 1, t // 2)
                if 0 < t < VECTOR_B_SLOT and has_next:
                    interleave_b(act, j + 1, *B_PIECES[t])
                if t == PACK - 1 and has_next:
                    scale_state(j + 1, 0)


        bank_tags = ["s00", "s01", "s10", "s11", "p0", "p1", "o0", "o1"]
        banks = [(a, half) for half in range(2) for a in range(MT)]
        early, late = banks[:6], banks[6:]
        left, right = banks[:MT], banks[MT:]
        y_banks = {}

        def multiply_state(r, j, todo, start=False, stop=False):
            for a, half in todo:
                if start:
                    y_banks[a, half] = psum.tile([P, W], F32, tag=bank_tags[banks.index((a, half))], name="y_bank")
                matmul_mx(y_banks[a, half][:], x_codes[j, r], a * P, c_codes[r, j, half], start, stop)

        def store_y(a, half):
            rows = ring.tile([P, W], F32, tag="rows", bufs=STORE_BUFS, name="y_rows")
            vec.tensor_tensor(out=rows[:], in0=y_banks[a, half][:], in1=skip[:, a, half * W:(half + 1) * W], op=Alu.add)
            nc.sync.dma_start(out=out_0[a * P:(a + 1) * P, half * W:(half + 1) * W], in_=rows[:])

        last = BLOCKS - 1
        load_c_re(last)
        add_inputs(last, PACK - 1)
        widen_c_re(2, 0)
        quantise_c(RE, 0, 1)
        interleave_x(last, RE)
        interleave_c(RE, 1, 0)
        quantise_c(IM, 2, 1)
        interleave_x(last, IM)
        interleave_c(RE, 1, 1)

        pairs = [(r, a) for r in (RE, IM) for a in (0, 2)]
        for i, (r, a) in enumerate(pairs):
            store_x(last, r, a)
            store_x(last, r, a + 1)
            if i == 1:
                widen_c_re(2, 1)
            if i < last:
                multiply_state(IM, i, early, start=(i == 0))
        quantise_x(last, RE)
        quantise_c(RE, 1, 0)
        quantise_x(last, IM)
        quantise_c(RE, 1, 1)
        for i in range(last):
            multiply_state(IM, i, late, start=(i == 0))
        multiply_state(RE, 0, banks)
        multiply_state(RE, 1, banks)

        interleave_c(RE, 2, 0)
        interleave_c(RE, 2, 1)
        widen_c_re(last, 0)
        widen_c_re(last, 1)
        interleave_c(IM, last, 1)
        quantise_c(RE, 2, 0)
        interleave_c(RE, last, 0)
        quantise_c(RE, 2, 1)
        multiply_state(RE, 2, banks)
        interleave_c(IM, last, 0)
        quantise_c(IM, last, 1)
        quantise_c(RE, last, 0)
        interleave_c(RE, last, 1)
        quantise_c(IM, last, 0)
        multiply_state(RE, last, left)
        multiply_state(IM, last, left, stop=True)
        quantise_c(RE, last, 1)
        multiply_state(IM, last, right)
        multiply_state(RE, last, right, stop=True)
        for a, half in banks:
            store_y(a, half)
